import numpy as np
import ml_dtypes


def mxq(x, axis, fmt="e4m3"):
    dtype, down = {"e4m3": (ml_dtypes.float8_e4m3fn, 7), "e5m2": (ml_dtypes.float8_e5m2, 14)}[fmt]
    v = np.moveaxis(np.asarray(x, np.float32).astype(ml_dtypes.bfloat16).astype(np.float64), axis, -1)
    blocks = v.reshape(v.shape[:-1] + (-1, 32))
    amax = np.abs(blocks).max(-1, keepdims=True)
    byte = np.maximum(np.where(amax > 0, np.frexp(amax)[1] - 1 + 127, 0) - down, 1)
    scale = np.exp2(byte - 127.0)
    codes = (blocks / scale).astype(np.float32).astype(dtype).astype(np.float64)
    return np.moveaxis((codes * scale).reshape(v.shape), -1, axis)


WIDE = False


def mx_kscale(k):
    if not WIDE:
        return np.ones(k)
    levels = np.array([10, -10, 5, -5, 0])
    a = np.random.permutation(np.resize(levels, k // 512 * 4)).reshape(k // 512, 4)
    idx = np.arange(k)
    return np.exp2(a[idx // 512, idx % 128 // 32])


BF16 = ml_dtypes.bfloat16


def bf(x):
    return np.asarray(x, np.float32).astype(BF16)


def f64(x):
    return np.asarray(x).astype(np.float64)


B, CIN, H, W, CK, CV, COUT, S = 2, 512, 32, 64, 256, 256, 512, 2
HP, WP = H // S, W // S
NW, L = S * S, HP * WP


def to_windows(t):
    c = t.shape[1]
    return t.reshape(B, c, S, HP, S, WP).transpose(0, 2, 4, 3, 5, 1).reshape(B, NW, L, c)


def setup_inputs():
    s = mx_kscale(CIN)
    return {"x": bf(np.random.standard_normal((B, CIN, H, W)) * s[None, :, None, None]),
            "q": bf(np.maximum(np.random.standard_normal((B, CK, H, W)) * 2.2, 0.0)),
            "k": bf(np.maximum(np.random.standard_normal((B, CK, H, W)) * 2.2, 0.0)),
            "v_w": bf(np.random.standard_normal((CV, CIN)) * 1.5 / np.sqrt(CIN) / s[None, :]),
            "v_b": bf(np.random.standard_normal(CV) * 0.3)}


def reference(x, q, k, v_w, v_b):
    v = (mxq(f64(v_w), 1, "e4m3") @ mxq(f64(x).reshape(B, CIN, H * W), 1, "e4m3")) + f64(v_b)[None, :, None]
    qw, kw, vw = to_windows(f64(q)), to_windows(f64(k)), to_windows(v.reshape(B, CV, H, W))
    sim = qw @ kw.transpose(0, 1, 3, 2) * CK ** -0.5
    e = np.exp(sim - sim.max(-1, keepdims=True))
    ctx = (mxq(e, 3, "e4m3") @ mxq(vw, 2, "e4m3")) / e.sum(-1, keepdims=True)
    return ctx.reshape(B, S, S, HP, WP, CV).transpose(0, 5, 1, 3, 2, 4).reshape(B, CV, H, W)

@@ -1,0 +1,257 @@
+from contextlib import ExitStack
+
+import concourse.mybir as mybir
+from concourse.masks import make_identity
+
+F32 = mybir.dt.float32
+BF16 = mybir.dt.bfloat16
+U32 = mybir.dt.uint32
+U8 = mybir.dt.uint8
+FP8X4 = mybir.dt.float8_e4m3fn_x4
+ADD = mybir.AluOpType.add
+MULT = mybir.AluOpType.mult
+MAX = mybir.AluOpType.max
+EXP = mybir.ActivationFunctionType.Exp
+FREE_AXIS = mybir.AxisListType.X
+
+P = 128
+PACK = 4
+IMAGES, CIN, CK, CV = 2, 512, 256, 256
+SPLIT = 2
+WIN_ROWS, WIN_COLS = 16, 32
+TOKENS = WIN_ROWS * WIN_COLS
+BAND = SPLIT * TOKENS
+N_BANDS = IMAGES * SPLIT
+N_WINDOWS = N_BANDS * SPLIT
+CK_TILES = CK // P
+CV_TILES = CV // P
+ROW_TILES = TOKENS // P
+HALF = TOKENS // 2
+
+FLOPS = 2 * IMAGES * CV * CIN * SPLIT * BAND + 2 * 2 * N_WINDOWS * TOKENS * TOKENS * CK
+
+
+def window_of(band_view, side):
+    if band_view.ndim == 2:
+        return band_view.rearrange("p (i d j) -> p d i j", d=SPLIT, j=WIN_COLS)[:, side]
+    return band_view.rearrange("p c (i d j) -> p d c i j", d=SPLIT, j=WIN_COLS)[:, side]
+
+
+def tile_pyramidselfattentionblock_pa_kernel(tc, x, q, k, v_w, v_b, out):
+    nc = tc.nc
+    with ExitStack() as ctx:
+        const = ctx.enter_context(tc.tile_pool(name="const", bufs=1))
+        maps = ctx.enter_context(tc.tile_pool(name="maps", bufs=N_BANDS))
+        ahead = ctx.enter_context(tc.tile_pool(name="ahead", bufs=3))
+        work = ctx.enter_context(tc.tile_pool(name="work", bufs=2))
+        rows = ctx.enter_context(tc.tile_pool(name="rows", bufs=2 * ROW_TILES))
+        sim_banks = ctx.enter_context(tc.psum_pool(name="sim_banks", bufs=3))
+        turn_banks = ctx.enter_context(tc.psum_pool(name="turn_banks", bufs=3))
+        mx_banks = ctx.enter_context(tc.psum_pool(name="mx_banks", bufs=2))
+
+        w_raw = const.tile([P, CV_TILES * CIN], BF16)
+        nc.sync.dma_start(
+            out=w_raw[:].rearrange("p (h c) -> p h c", h=CV_TILES),
+            in_=v_w.rearrange("(h p) c -> p h c", p=P),
+        )
+        bias = const.tile([P, CV], BF16)
+        nc.sync.dma_start(out=bias[:], in_=v_b.partition_broadcast(P))
+        q_bands, k_bands, x_bands = [], [], []
+        for band in range(N_BANDS):
+            image, pixels = band // SPLIT, slice((band % SPLIT) * BAND, (band % SPLIT + 1) * BAND)
+            q_raw = maps.tile([P, CK_TILES, BAND], BF16)
+            nc.sync.dma_start(out=q_raw[:], in_=q[image].rearrange("(c p) h w -> p c (h w)", p=P)[:, :, pixels])
+            k_raw = maps.tile([P, CK_TILES, BAND], BF16)
+            nc.sync.dma_start(out=k_raw[:], in_=k[image].rearrange("(c p) h w -> p c (h w)", p=P)[:, :, pixels])
+            x_raw = maps.tile([P, PACK, BAND], BF16)
+            nc.sync.dma_start(out=x_raw[:], in_=x[image].rearrange("(p j) h w -> p j (h w)", j=PACK)[:, :, pixels])
+            q_bands.append(q_raw)
+            k_bands.append(k_raw)
+            x_bands.append(x_raw)
+
+        ident_f32 = const.tile([P, P], F32)
+        make_identity(nc, ident_f32[:])
+        ident_bf16 = const.tile([P, P], BF16)
+        make_identity(nc, ident_bf16[:])
+
+        w_words = w_raw[:].bitcast(F32).rearrange("p (h w u) -> p h u w", h=CV_TILES, u=2)
+        w_turned = turn_banks.tile([P, 2, CV], F32, tag="turn")
+        for h in range(CV_TILES):
+            for u in range(2):
+                nc.tensor.transpose(out=w_turned[:, u, h * P : (h + 1) * P], in_=w_words[:, h, u, :], identity=ident_f32[:])
+        w_grouped = const.tile([P, CV * PACK], BF16, align_bytes=64)
+        nc.vector.tensor_copy(
+            out=w_grouped[:].bitcast(F32).rearrange("p (o u) -> p o u", u=2),
+            in_=w_turned[:].rearrange("p u o -> p o u"),
+        )
+        w_codes = const.tile([P, CV], U32, align_bytes=64)
+        w_scales = const.tile([P, CV], U8, align_bytes=64)
+        nc.vector.quantize_mx(out=w_codes[:].bitcast(FP8X4), scales=w_scales[:], in_=w_grouped[:])
+
+        state = {}
+
+        def prepare(win):
+            band, side = win // SPLIT, win % SPLIT
+            q_win = ahead.tile([P, CK_TILES, TOKENS], BF16)
+            nc.gpsimd.tensor_scalar(
+                out=q_win[:].rearrange("p c (i j) -> p c i j", j=WIN_COLS),
+                in0=window_of(q_bands[band][:], side),
+                scalar1=CK**-0.5,
+                scalar2=0.0,
+                op0=MULT,
+                op1=ADD,
+            )
+            x_grouped = ahead.tile([P, TOKENS, PACK], BF16, align_bytes=64)
+            nc.gpsimd.tensor_scalar(
+                out=x_grouped[:].rearrange("p (i j) c -> p i j c", j=WIN_COLS),
+                in0=window_of(x_bands[band][:], side).rearrange("p c i j -> p i j c"),
+                scalar1=1.0,
+                scalar2=0.0,
+                op0=MULT,
+                op1=ADD,
+            )
+            state[("q", win)] = q_win
+            state[("x", win)] = x_grouped
+
+        def values(win):
+            x_grouped = state[("x", win)]
+            x_codes = ahead.tile([P, TOKENS], U32, align_bytes=64)
+            x_scales = ahead.tile([P, TOKENS], U8, align_bytes=64)
+            nc.vector.quantize_mx(
+                out=x_codes[:].bitcast(FP8X4), scales=x_scales[:], in_=x_grouped[:].rearrange("p l c -> p (l c)")
+            )
+            v_grouped = work.tile([P, CV_TILES, P, PACK], BF16, align_bytes=64)
+            for h in range(CV_TILES):
+                channels = slice(h * P, (h + 1) * P)
+                v_acc = mx_banks.tile([P, PACK, P], F32, tag="mx")
+                for t in range(PACK):
+                    keys = slice(t * P, (t + 1) * P)
+                    nc.tensor.matmul_mx(
+                        out=v_acc[:, t, :],
+                        lhsT=x_codes[:, keys].bitcast(FP8X4),
+                        lhsT_scale=x_scales[:, keys],
+                        rhs=w_codes[:, channels].bitcast(FP8X4),
+                        rhs_scale=w_scales[:, channels],
+                        start=True,
+                        stop=True,
+                    )
+                nc.vector.tensor_tensor(
+                    out=v_grouped[:, h],
+                    in0=v_acc[:].rearrange("p t o -> p o t"),
+                    in1=bias[:, channels].unsqueeze(2).to_broadcast([P, P, PACK]),
+                    op=ADD,
+                )
+            v_codes = ahead.tile([P, CV], U32, align_bytes=64)
+            v_scales = ahead.tile([P, CV], U8, align_bytes=64)
+            nc.vector.quantize_mx(
+                out=v_codes[:].bitcast(FP8X4), scales=v_scales[:], in_=v_grouped[:].rearrange("p h o t -> p (h o t)")
+            )
+            state[("v", win)] = (v_codes, v_scales)
+
+        def scores(win):
+            band, side = win // SPLIT, win % SPLIT
+            q_win = state[("q", win)]
+            k_win = window_of(k_bands[band][:], side)
+            neg_max = work.tile([P, ROW_TILES], F32)
+            row_sum = work.tile([P, ROW_TILES], F32)
+            e_tiles = []
+            for r in range(ROW_TILES):
+                sim = sim_banks.tile([P, TOKENS], F32)
+                for c in range(CK_TILES):
+                    nc.tensor.matmul(
+                        out=sim[:].rearrange("p (i j) -> p i j", j=WIN_COLS),
+                        lhsT=q_win[:, c, r * P : (r + 1) * P],
+                        rhs=k_win[:, c],
+                        start=(c == 0),
+                        stop=(c == CK_TILES - 1),
+                    )
+                nc.vector.tensor_reduce(out=neg_max[:, r : r + 1], in_=sim[:], axis=FREE_AXIS, op=MAX, negate=True)
+                e_rows = rows.tile([P, TOKENS], BF16)
+                nc.scalar.activation(
+                    out=e_rows[:],
+                    in_=sim[:],
+                    func=EXP,
+                    bias=neg_max[:, r : r + 1],
+                    scale=1.0,
+                    accum_out=row_sum[:, r : r + 1],
+                )
+                e_tiles.append(e_rows)
+            state[("e", win)] = e_tiles
+            state[("sum", win)] = row_sum
+
+        def turn(win):
+            e_tiles = state[("e", win)]
+            e_grouped = work.tile([P, TOKENS, PACK], BF16, align_bytes=64)
+            for half in range(TOKENS // HALF):
+                e_turned = turn_banks.tile([P, PACK, HALF], BF16, tag="turn")
+                for r in range(HALF // P):
+                    for t in range(PACK):
+                        nc.tensor.transpose(
+                            out=e_turned[:, t, r * P : (r + 1) * P],
+                            in_=e_tiles[half * (HALF // P) + r][:, t * P : (t + 1) * P],
+                            identity=ident_bf16[:],
+                        )
+                nc.scalar.copy(
+                    out=e_grouped[:, half * HALF : (half + 1) * HALF, :], in_=e_turned[:].rearrange("p t l -> p l t")
+                )
+            e_codes = work.tile([P, TOKENS], U32, align_bytes=64)
+            e_scales = work.tile([P, TOKENS], U8, align_bytes=64)
+            nc.vector.quantize_mx(
+                out=e_codes[:].bitcast(FP8X4), scales=e_scales[:], in_=e_grouped[:].rearrange("p l t -> p (l t)")
+            )
+            state[("ec", win)] = (e_codes, e_scales)
+
+        def context(win):
+            band, side = win // SPLIT, win % SPLIT
+            v_codes, v_scales = state[("v", win)]
+            e_codes, e_scales = state[("ec", win)]
+            inv_sum = work.tile([P, ROW_TILES], F32)
+            nc.vector.reciprocal(out=inv_sum[:], in_=state[("sum", win)][:])
+            inv_turned = turn_banks.tile([P, TOKENS], F32, tag="turn")
+            for r in range(ROW_TILES):
+                nc.tensor.transpose(
+                    out=inv_turned[:, r * P : (r + 1) * P],
+                    in_=inv_sum[:, r : r + 1].to_broadcast([P, P]),
+                    identity=ident_f32[:],
+                )
+            inv_all = work.tile([P, TOKENS], F32)
+            nc.scalar.copy(out=inv_all[:], in_=inv_turned[:])
+            if side == 0:
+                for h in range(CV_TILES):
+                    state[("out", h)] = work.tile([P, BAND], F32, name="out_band%d" % h)
+            for h in range(CV_TILES):
+                channels = slice(h * P, (h + 1) * P)
+                ctx_acc = mx_banks.tile([P, TOKENS], F32, tag="mx")
+                nc.tensor.matmul_mx(
+                    out=ctx_acc[:],
+                    lhsT=v_codes[:, channels].bitcast(FP8X4),
+                    lhsT_scale=v_scales[:, channels],
+                    rhs=e_codes[:].bitcast(FP8X4),
+                    rhs_scale=e_scales[:],
+                    start=True,
+                    stop=True,
+                )
+                nc.vector.tensor_tensor(
+                    out=window_of(state[("out", h)][:], side),
+                    in0=ctx_acc[:].rearrange("p (i j) -> p i j", j=WIN_COLS),
+                    in1=inv_all[:].rearrange("p (i j) -> p i j", j=WIN_COLS),
+                    op=MULT,
+                )
+                if side == SPLIT - 1:
+                    image, first_row = band // SPLIT, (band % SPLIT) * WIN_ROWS
+                    nc.sync.dma_start(
+                        out=out[image, channels, first_row : first_row + WIN_ROWS, :].rearrange("o h w -> o (h w)"),
+                        in_=state[("out", h)][:],
+                    )
+
+        prepare(0)
+        values(0)
+        prepare(1)
+        for win in range(N_WINDOWS):
+            scores(win)
+            if win + 2 < N_WINDOWS:
+                prepare(win + 2)
+            if win + 1 < N_WINDOWS:
+                values(win + 1)
+            turn(win)
+            context(win)

@@ -27,6 +27,8 @@ CK_TILES = CK // P
 CV_TILES = CV // P
 ROW_TILES = TOKENS // P
 HALF = TOKENS // 2
+VECTOR_ROWS = 6
+RUN = 4
 
 FLOPS = 2 * IMAGES * CV * CIN * SPLIT * BAND + 2 * 2 * N_WINDOWS * TOKENS * TOKENS * CK
 
@@ -93,22 +95,23 @@ def tile_pyramidselfattentionblock_pa_kernel(tc, x, q, k, v_w, v_b, out):
         def prepare(win):
             band, side = win // SPLIT, win % SPLIT
             q_win = ahead.tile([P, CK_TILES, TOKENS], BF16)
-            nc.gpsimd.tensor_scalar(
+            nc.vector.tensor_scalar(
                 out=q_win[:].rearrange("p c (i j) -> p c i j", j=WIN_COLS),
                 in0=window_of(q_bands[band][:], side),
                 scalar1=CK**-0.5,
-                scalar2=0.0,
+                scalar2=None,
                 op0=MULT,
-                op1=ADD,
             )
+            x_win = window_of(x_bands[band][:], side)
             x_grouped = ahead.tile([P, TOKENS, PACK], BF16, align_bytes=64)
-            nc.gpsimd.tensor_scalar(
-                out=x_grouped[:].rearrange("p (i j) c -> p i j c", j=WIN_COLS),
-                in0=window_of(x_bands[band][:], side).rearrange("p c i j -> p i j c"),
-                scalar1=1.0,
-                scalar2=0.0,
-                op0=MULT,
-                op1=ADD,
+            split = VECTOR_ROWS * WIN_COLS
+            nc.vector.tensor_copy(
+                out=x_grouped[:, :split, :].rearrange("p (i g r) c -> p i g c r", g=WIN_COLS // RUN, r=RUN),
+                in_=x_win[:, :, :VECTOR_ROWS, :].rearrange("p c i (g r) -> p i g c r", r=RUN),
+            )
+            nc.scalar.copy(
+                out=x_grouped[:, split:, :].rearrange("p (i j) c -> p i j c", j=WIN_COLS),
+                in_=x_win[:, :, VECTOR_ROWS:, :].rearrange("p c i j -> p i j c"),
             )
             state[("q", win)] = q_win
             state[("x", win)] = x_grouped

@@ -28,6 +28,7 @@ CV_TILES = CV // P
 ROW_TILES = TOKENS // P
 HALF = TOKENS // 2
 VECTOR_ROWS = 6
+SCALAR_ROWS = (WIN_ROWS - VECTOR_ROWS) // 2
 RUN = 4
 
 FLOPS = 2 * IMAGES * CV * CIN * SPLIT * BAND + 2 * 2 * N_WINDOWS * TOKENS * TOKENS * CK
@@ -42,14 +43,14 @@ def window_of(band_view, side):
 def tile_pyramidselfattentionblock_pa_kernel(tc, x, q, k, v_w, v_b, out):
     nc = tc.nc
     with ExitStack() as ctx:
+        ctx.enter_context(tc.manual_schedule())
         const = ctx.enter_context(tc.tile_pool(name="const", bufs=1))
         maps = ctx.enter_context(tc.tile_pool(name="maps", bufs=N_BANDS))
-        ahead = ctx.enter_context(tc.tile_pool(name="ahead", bufs=3))
-        work = ctx.enter_context(tc.tile_pool(name="work", bufs=2))
+        work = ctx.enter_context(tc.tile_pool(name="work", bufs=3))
         rows = ctx.enter_context(tc.tile_pool(name="rows", bufs=2 * ROW_TILES))
         sim_banks = ctx.enter_context(tc.psum_pool(name="sim_banks", bufs=3))
-        turn_banks = ctx.enter_context(tc.psum_pool(name="turn_banks", bufs=3))
-        mx_banks = ctx.enter_context(tc.psum_pool(name="mx_banks", bufs=2))
+        turn_banks = ctx.enter_context(tc.psum_pool(name="turn_banks", bufs=2))
+        mx_banks = ctx.enter_context(tc.psum_pool(name="mx_banks", bufs=3))
 
         w_raw = const.tile([P, CV_TILES * CIN], BF16)
         nc.sync.dma_start(
@@ -61,12 +62,12 @@ def tile_pyramidselfattentionblock_pa_kernel(tc, x, q, k, v_w, v_b, out):
         q_bands, k_bands, x_bands = [], [], []
         for band in range(N_BANDS):
             image, pixels = band // SPLIT, slice((band % SPLIT) * BAND, (band % SPLIT + 1) * BAND)
+            x_raw = maps.tile([P, PACK, BAND], BF16)
+            nc.sync.dma_start(out=x_raw[:], in_=x[image].rearrange("(p j) h w -> p j (h w)", j=PACK)[:, :, pixels])
             q_raw = maps.tile([P, CK_TILES, BAND], BF16)
             nc.sync.dma_start(out=q_raw[:], in_=q[image].rearrange("(c p) h w -> p c (h w)", p=P)[:, :, pixels])
             k_raw = maps.tile([P, CK_TILES, BAND], BF16)
             nc.sync.dma_start(out=k_raw[:], in_=k[image].rearrange("(c p) h w -> p c (h w)", p=P)[:, :, pixels])
-            x_raw = maps.tile([P, PACK, BAND], BF16)
-            nc.sync.dma_start(out=x_raw[:], in_=x[image].rearrange("(p j) h w -> p j (h w)", j=PACK)[:, :, pixels])
             q_bands.append(q_raw)
             k_bands.append(k_raw)
             x_bands.append(x_raw)
@@ -90,171 +91,235 @@ def tile_pyramidselfattentionblock_pa_kernel(tc, x, q, k, v_w, v_b, out):
         w_scales = const.tile([P, CV], U8, align_bytes=64)
         nc.vector.quantize_mx(out=w_codes[:].bitcast(FP8X4), scales=w_scales[:], in_=w_grouped[:])
 
-        state = {}
+        tiles = {}
 
-        def prepare(win):
-            band, side = win // SPLIT, win % SPLIT
-            q_win = ahead.tile([P, CK_TILES, TOKENS], BF16)
+        def q_window(win):
+            q_win = work.tile([P, CK_TILES, TOKENS], BF16)
             nc.vector.tensor_scalar(
                 out=q_win[:].rearrange("p c (i j) -> p c i j", j=WIN_COLS),
-                in0=window_of(q_bands[band][:], side),
+                in0=window_of(q_bands[win // SPLIT][:], win % SPLIT),
                 scalar1=CK**-0.5,
                 scalar2=None,
                 op0=MULT,
             )
-            x_win = window_of(x_bands[band][:], side)
-            x_grouped = ahead.tile([P, TOKENS, PACK], BF16, align_bytes=64)
-            split = VECTOR_ROWS * WIN_COLS
+            tiles[("q", win)] = q_win
+
+        def x_scalar(win, part):
+            if part == 0:
+                tiles[("x", win)] = work.tile([P, TOKENS, PACK], BF16, name="x_grouped", align_bytes=64)
+            first = VECTOR_ROWS + part * SCALAR_ROWS
+            x_win = window_of(x_bands[win // SPLIT][:], win % SPLIT)
+            nc.scalar.copy(
+                out=tiles[("x", win)][:, first * WIN_COLS : (first + SCALAR_ROWS) * WIN_COLS, :].rearrange(
+                    "p (i j) c -> p i j c", j=WIN_COLS
+                ),
+                in_=x_win[:, :, first : first + SCALAR_ROWS, :].rearrange("p c i j -> p i j c"),
+            )
+
+        def x_vector(win):
+            x_win = window_of(x_bands[win // SPLIT][:], win % SPLIT)
             nc.vector.tensor_copy(
-                out=x_grouped[:, :split, :].rearrange("p (i g r) c -> p i g c r", g=WIN_COLS // RUN, r=RUN),
+                out=tiles[("x", win)][:, : VECTOR_ROWS * WIN_COLS, :].rearrange(
+                    "p (i g r) c -> p i g c r", g=WIN_COLS // RUN, r=RUN
+                ),
                 in_=x_win[:, :, :VECTOR_ROWS, :].rearrange("p c i (g r) -> p i g c r", r=RUN),
             )
-            nc.scalar.copy(
-                out=x_grouped[:, split:, :].rearrange("p (i j) c -> p i j c", j=WIN_COLS),
-                in_=x_win[:, :, VECTOR_ROWS:, :].rearrange("p c i j -> p i j c"),
-            )
-            state[("q", win)] = q_win
-            state[("x", win)] = x_grouped
 
-        def values(win):
-            x_grouped = state[("x", win)]
-            x_codes = ahead.tile([P, TOKENS], U32, align_bytes=64)
-            x_scales = ahead.tile([P, TOKENS], U8, align_bytes=64)
+        def x_quantise(win):
+            x_codes = work.tile([P, TOKENS], U32, align_bytes=64)
+            x_scales = work.tile([P, TOKENS], U8, align_bytes=64)
             nc.vector.quantize_mx(
-                out=x_codes[:].bitcast(FP8X4), scales=x_scales[:], in_=x_grouped[:].rearrange("p l c -> p (l c)")
+                out=x_codes[:].bitcast(FP8X4), scales=x_scales[:], in_=tiles[("x", win)][:].rearrange("p l c -> p (l c)")
             )
-            v_grouped = work.tile([P, CV_TILES, P, PACK], BF16, align_bytes=64)
-            for h in range(CV_TILES):
-                channels = slice(h * P, (h + 1) * P)
-                v_acc = mx_banks.tile([P, PACK, P], F32, tag="mx")
+            tiles[("xq", win)] = (x_codes, x_scales)
+
+        def v_matmul(win, h):
+            x_codes, x_scales = tiles[("xq", win)]
+            channels = slice(h * P, (h + 1) * P)
+            v_acc = mx_banks.tile([P, PACK, P], F32, tag="mx")
+            for t in range(PACK):
+                keys = slice(t * P, (t + 1) * P)
+                nc.tensor.matmul_mx(
+                    out=v_acc[:, t, :],
+                    lhsT=x_codes[:, keys].bitcast(FP8X4),
+                    lhsT_scale=x_scales[:, keys],
+                    rhs=w_codes[:, channels].bitcast(FP8X4),
+                    rhs_scale=w_scales[:, channels],
+                    start=True,
+                    stop=True,
+                )
+            tiles[("vacc", win, h)] = v_acc
+
+        def v_bias(win, h):
+            if h == 0:
+                tiles[("vg", win)] = work.tile([P, CV_TILES, P, PACK], BF16, name="v_grouped", align_bytes=64)
+            nc.vector.tensor_tensor(
+                out=tiles[("vg", win)][:, h],
+                in0=tiles[("vacc", win, h)][:].rearrange("p t o -> p o t"),
+                in1=bias[:, h * P : (h + 1) * P].unsqueeze(2).to_broadcast([P, P, PACK]),
+                op=ADD,
+            )
+
+        def v_quantise(win):
+            v_codes = work.tile([P, CV], U32, align_bytes=64)
+            v_scales = work.tile([P, CV], U8, align_bytes=64)
+            nc.vector.quantize_mx(
+                out=v_codes[:].bitcast(FP8X4), scales=v_scales[:], in_=tiles[("vg", win)][:].rearrange("p h o t -> p (h o t)")
+            )
+            tiles[("vq", win)] = (v_codes, v_scales)
+
+        def sim_matmul(win, r):
+            k_win = window_of(k_bands[win // SPLIT][:], win % SPLIT)
+            sim = sim_banks.tile([P, TOKENS], F32)
+            for c in range(CK_TILES):
+                nc.tensor.matmul(
+                    out=sim[:].rearrange("p (i j) -> p i j", j=WIN_COLS),
+                    lhsT=tiles[("q", win)][:, c, r * P : (r + 1) * P],
+                    rhs=k_win[:, c],
+                    start=(c == 0),
+                    stop=(c == CK_TILES - 1),
+                )
+            tiles[("sim", win, r)] = sim
+
+        def row_max(win, r):
+            if r == 0:
+                tiles[("max", win)] = work.tile([P, ROW_TILES], F32, name="neg_max")
+            nc.vector.tensor_reduce(
+                out=tiles[("max", win)][:, r : r + 1], in_=tiles[("sim", win, r)][:], axis=FREE_AXIS, op=MAX, negate=True
+            )
+
+        def exponent(win, r):
+            if r == 0:
+                tiles[("sum", win)] = work.tile([P, ROW_TILES], F32, name="row_sum")
+            e_rows = rows.tile([P, TOKENS], BF16)
+            nc.scalar.activation(
+                out=e_rows[:],
+                in_=tiles[("sim", win, r)][:],
+                func=EXP,
+                bias=tiles[("max", win)][:, r : r + 1],
+                scale=1.0,
+                accum_out=tiles[("sum", win)][:, r : r + 1],
+            )
+            tiles[("e", win, r)] = e_rows
+
+        def e_turn(win, half):
+            e_turned = turn_banks.tile([P, PACK, HALF], BF16, tag="turn")
+            for r in range(HALF // P):
                 for t in range(PACK):
-                    keys = slice(t * P, (t + 1) * P)
-                    nc.tensor.matmul_mx(
-                        out=v_acc[:, t, :],
-                        lhsT=x_codes[:, keys].bitcast(FP8X4),
-                        lhsT_scale=x_scales[:, keys],
-                        rhs=w_codes[:, channels].bitcast(FP8X4),
-                        rhs_scale=w_scales[:, channels],
-                        start=True,
-                        stop=True,
+                    nc.tensor.transpose(
+                        out=e_turned[:, t, r * P : (r + 1) * P],
+                        in_=tiles[("e", win, half * (HALF // P) + r)][:, t * P : (t + 1) * P],
+                        identity=ident_bf16[:],
                     )
-                nc.vector.tensor_tensor(
-                    out=v_grouped[:, h],
-                    in0=v_acc[:].rearrange("p t o -> p o t"),
-                    in1=bias[:, channels].unsqueeze(2).to_broadcast([P, P, PACK]),
-                    op=ADD,
-                )
-            v_codes = ahead.tile([P, CV], U32, align_bytes=64)
-            v_scales = ahead.tile([P, CV], U8, align_bytes=64)
-            nc.vector.quantize_mx(
-                out=v_codes[:].bitcast(FP8X4), scales=v_scales[:], in_=v_grouped[:].rearrange("p h o t -> p (h o t)")
+            tiles[("et", win, half)] = e_turned
+
+        def e_copy(win, half):
+            if half == 0:
+                tiles[("eg", win)] = work.tile([P, TOKENS, PACK], BF16, name="e_grouped", align_bytes=64)
+            nc.scalar.copy(
+                out=tiles[("eg", win)][:, half * HALF : (half + 1) * HALF, :],
+                in_=tiles[("et", win, half)][:].rearrange("p t l -> p l t"),
             )
-            state[("v", win)] = (v_codes, v_scales)
 
-        def scores(win):
-            band, side = win // SPLIT, win % SPLIT
-            q_win = state[("q", win)]
-            k_win = window_of(k_bands[band][:], side)
-            neg_max = work.tile([P, ROW_TILES], F32)
-            row_sum = work.tile([P, ROW_TILES], F32)
-            e_tiles = []
-            for r in range(ROW_TILES):
-                sim = sim_banks.tile([P, TOKENS], F32)
-                for c in range(CK_TILES):
-                    nc.tensor.matmul(
-                        out=sim[:].rearrange("p (i j) -> p i j", j=WIN_COLS),
-                        lhsT=q_win[:, c, r * P : (r + 1) * P],
-                        rhs=k_win[:, c],
-                        start=(c == 0),
-                        stop=(c == CK_TILES - 1),
-                    )
-                nc.vector.tensor_reduce(out=neg_max[:, r : r + 1], in_=sim[:], axis=FREE_AXIS, op=MAX, negate=True)
-                e_rows = rows.tile([P, TOKENS], BF16)
-                nc.scalar.activation(
-                    out=e_rows[:],
-                    in_=sim[:],
-                    func=EXP,
-                    bias=neg_max[:, r : r + 1],
-                    scale=1.0,
-                    accum_out=row_sum[:, r : r + 1],
-                )
-                e_tiles.append(e_rows)
-            state[("e", win)] = e_tiles
-            state[("sum", win)] = row_sum
-
-        def turn(win):
-            e_tiles = state[("e", win)]
-            e_grouped = work.tile([P, TOKENS, PACK], BF16, align_bytes=64)
-            for half in range(TOKENS // HALF):
-                e_turned = turn_banks.tile([P, PACK, HALF], BF16, tag="turn")
-                for r in range(HALF // P):
-                    for t in range(PACK):
-                        nc.tensor.transpose(
-                            out=e_turned[:, t, r * P : (r + 1) * P],
-                            in_=e_tiles[half * (HALF // P) + r][:, t * P : (t + 1) * P],
-                            identity=ident_bf16[:],
-                        )
-                nc.scalar.copy(
-                    out=e_grouped[:, half * HALF : (half + 1) * HALF, :], in_=e_turned[:].rearrange("p t l -> p l t")
-                )
+        def e_quantise(win):
             e_codes = work.tile([P, TOKENS], U32, align_bytes=64)
             e_scales = work.tile([P, TOKENS], U8, align_bytes=64)
             nc.vector.quantize_mx(
-                out=e_codes[:].bitcast(FP8X4), scales=e_scales[:], in_=e_grouped[:].rearrange("p l t -> p (l t)")
+                out=e_codes[:].bitcast(FP8X4), scales=e_scales[:], in_=tiles[("eg", win)][:].rearrange("p l t -> p (l t)")
             )
-            state[("ec", win)] = (e_codes, e_scales)
+            tiles[("eq", win)] = (e_codes, e_scales)
 
-        def context(win):
-            band, side = win // SPLIT, win % SPLIT
-            v_codes, v_scales = state[("v", win)]
-            e_codes, e_scales = state[("ec", win)]
+        def sum_invert(win):
             inv_sum = work.tile([P, ROW_TILES], F32)
-            nc.vector.reciprocal(out=inv_sum[:], in_=state[("sum", win)][:])
+            nc.vector.reciprocal(out=inv_sum[:], in_=tiles[("sum", win)][:])
+            tiles[("inv", win)] = inv_sum
+
+        def inv_turn(win):
             inv_turned = turn_banks.tile([P, TOKENS], F32, tag="turn")
             for r in range(ROW_TILES):
                 nc.tensor.transpose(
                     out=inv_turned[:, r * P : (r + 1) * P],
-                    in_=inv_sum[:, r : r + 1].to_broadcast([P, P]),
+                    in_=tiles[("inv", win)][:, r : r + 1].to_broadcast([P, P]),
                     identity=ident_f32[:],
                 )
-            inv_all = work.tile([P, TOKENS], F32)
-            nc.scalar.copy(out=inv_all[:], in_=inv_turned[:])
-            if side == 0:
-                for h in range(CV_TILES):
-                    state[("out", h)] = work.tile([P, BAND], F32, name="out_band%d" % h)
-            for h in range(CV_TILES):
-                channels = slice(h * P, (h + 1) * P)
-                ctx_acc = mx_banks.tile([P, TOKENS], F32, tag="mx")
-                nc.tensor.matmul_mx(
-                    out=ctx_acc[:],
-                    lhsT=v_codes[:, channels].bitcast(FP8X4),
-                    lhsT_scale=v_scales[:, channels],
-                    rhs=e_codes[:].bitcast(FP8X4),
-                    rhs_scale=e_scales[:],
-                    start=True,
-                    stop=True,
-                )
-                nc.vector.tensor_tensor(
-                    out=window_of(state[("out", h)][:], side),
-                    in0=ctx_acc[:].rearrange("p (i j) -> p i j", j=WIN_COLS),
-                    in1=inv_all[:].rearrange("p (i j) -> p i j", j=WIN_COLS),
-                    op=MULT,
-                )
-                if side == SPLIT - 1:
-                    image, first_row = band // SPLIT, (band % SPLIT) * WIN_ROWS
-                    nc.sync.dma_start(
-                        out=out[image, channels, first_row : first_row + WIN_ROWS, :].rearrange("o h w -> o (h w)"),
-                        in_=state[("out", h)][:],
-                    )
+            tiles[("invt", win)] = inv_turned
 
-        prepare(0)
-        values(0)
-        prepare(1)
-        for win in range(N_WINDOWS):
-            scores(win)
-            if win + 2 < N_WINDOWS:
-                prepare(win + 2)
-            if win + 1 < N_WINDOWS:
-                values(win + 1)
-            turn(win)
-            context(win)
+        def inv_copy(win):
+            inv_all = work.tile([P, TOKENS], F32)
+            nc.scalar.copy(out=inv_all[:], in_=tiles[("invt", win)][:])
+            tiles[("inva", win)] = inv_all
+
+        def ctx_matmul(win, h):
+            v_codes, v_scales = tiles[("vq", win)]
+            e_codes, e_scales = tiles[("eq", win)]
+            ctx_acc = mx_banks.tile([P, TOKENS], F32, tag="mx")
+            nc.tensor.matmul_mx(
+                out=ctx_acc[:],
+                lhsT=v_codes[:, h * P : (h + 1) * P].bitcast(FP8X4),
+                lhsT_scale=v_scales[:, h * P : (h + 1) * P],
+                rhs=e_codes[:].bitcast(FP8X4),
+                rhs_scale=e_scales[:],
+                start=True,
+                stop=True,
+            )
+            tiles[("ctx", win, h)] = ctx_acc
+
+        def ctx_scale(win, h):
+            band, side = win // SPLIT, win % SPLIT
+            if side == 0:
+                tiles[("out", band, h)] = work.tile([P, BAND], F32, name="out_band%d" % h)
+            nc.vector.tensor_tensor(
+                out=window_of(tiles[("out", band, h)][:], side),
+                in0=tiles[("ctx", win, h)][:].rearrange("p (i j) -> p i j", j=WIN_COLS),
+                in1=tiles[("inva", win)][:].rearrange("p (i j) -> p i j", j=WIN_COLS),
+                op=MULT,
+            )
+            if side == SPLIT - 1:
+                image, first_row = band // SPLIT, (band % SPLIT) * WIN_ROWS
+                nc.sync.dma_start(
+                    out=out[image, h * P : (h + 1) * P, first_row : first_row + WIN_ROWS, :].rearrange("o h w -> o (h w)"),
+                    in_=tiles[("out", band, h)][:],
+                )
+
+        def run(stage, win, *args):
+            if 0 <= win < N_WINDOWS:
+                stage(win, *args)
+
+        for c in range(-2, N_WINDOWS + 2):
+            run(sim_matmul, c, 1)
+            run(ctx_matmul, c - 2, 0)
+            run(ctx_matmul, c - 2, 1)
+            run(row_max, c, 0)
+            run(v_bias, c, 1)
+            run(q_window, c + 1)
+            run(exponent, c - 1, 3)
+            run(inv_copy, c - 2)
+            run(e_copy, c - 1, 0)
+
+            run(sim_matmul, c, 2)
+            run(e_turn, c - 1, 1)
+            run(row_max, c, 1)
+            run(ctx_scale, c - 2, 0)
+            run(x_quantise, c + 1)
+            run(exponent, c, 0)
+            run(x_scalar, c + 2, 0)
+
+            run(sim_matmul, c, 3)
+            run(v_matmul, c + 1, 0)
+            run(v_matmul, c + 1, 1)
+            run(row_max, c, 2)
+            run(ctx_scale, c - 2, 1)
+            run(v_quantise, c)
+            run(sum_invert, c - 1)
+            run(x_vector, c + 2)
+            run(exponent, c, 1)
+            run(e_copy, c - 1, 1)
+
+            run(sim_matmul, c + 1, 0)
+            run(e_turn, c, 0)
+            run(inv_turn, c - 1)
+            run(row_max, c, 3)
+            run(e_quantise, c - 1)
+            run(v_bias, c + 1, 0)
+            run(exponent, c, 2)
+            run(x_scalar, c + 2, 1)

@@ -27,9 +27,6 @@ CK_TILES = CK // P
 CV_TILES = CV // P
 ROW_TILES = TOKENS // P
 HALF = TOKENS // 2
-VECTOR_ROWS = 6
-SCALAR_ROWS = (WIN_ROWS - VECTOR_ROWS) // 2
-RUN = 4
 
 FLOPS = 2 * IMAGES * CV * CIN * SPLIT * BAND + 2 * 2 * N_WINDOWS * TOKENS * TOKENS * CK
 
@@ -47,6 +44,8 @@ def tile_pyramidselfattentionblock_pa_kernel(tc, x, q, k, v_w, v_b, out):
         const = ctx.enter_context(tc.tile_pool(name="const", bufs=1))
         maps = ctx.enter_context(tc.tile_pool(name="maps", bufs=N_BANDS))
         work = ctx.enter_context(tc.tile_pool(name="work", bufs=3))
+        q_pool = ctx.enter_context(tc.tile_pool(name="q_pool", bufs=4))
+        x_pool = ctx.enter_context(tc.tile_pool(name="x_pool", bufs=1))
         rows = ctx.enter_context(tc.tile_pool(name="rows", bufs=2 * ROW_TILES))
         sim_banks = ctx.enter_context(tc.psum_pool(name="sim_banks", bufs=3))
         turn_banks = ctx.enter_context(tc.psum_pool(name="turn_banks", bufs=2))
@@ -62,12 +61,12 @@ def tile_pyramidselfattentionblock_pa_kernel(tc, x, q, k, v_w, v_b, out):
         q_bands, k_bands, x_bands = [], [], []
         for band in range(N_BANDS):
             image, pixels = band // SPLIT, slice((band % SPLIT) * BAND, (band % SPLIT + 1) * BAND)
-            x_raw = maps.tile([P, PACK, BAND], BF16)
-            nc.sync.dma_start(out=x_raw[:], in_=x[image].rearrange("(p j) h w -> p j (h w)", j=PACK)[:, :, pixels])
             q_raw = maps.tile([P, CK_TILES, BAND], BF16)
             nc.sync.dma_start(out=q_raw[:], in_=q[image].rearrange("(c p) h w -> p c (h w)", p=P)[:, :, pixels])
             k_raw = maps.tile([P, CK_TILES, BAND], BF16)
             nc.sync.dma_start(out=k_raw[:], in_=k[image].rearrange("(c p) h w -> p c (h w)", p=P)[:, :, pixels])
+            x_raw = maps.tile([P, PACK, BAND], BF16)
+            nc.sync.dma_start(out=x_raw[:], in_=x[image].rearrange("(p j) h w -> p j (h w)", j=PACK)[:, :, pixels])
             q_bands.append(q_raw)
             k_bands.append(k_raw)
             x_bands.append(x_raw)
@@ -94,36 +93,28 @@ def tile_pyramidselfattentionblock_pa_kernel(tc, x, q, k, v_w, v_b, out):
         tiles = {}
 
         def q_window(win):
-            q_win = work.tile([P, CK_TILES, TOKENS], BF16)
-            nc.vector.tensor_scalar(
+            q_win = q_pool.tile([P, CK_TILES, TOKENS], BF16)
+            nc.gpsimd.tensor_scalar(
                 out=q_win[:].rearrange("p c (i j) -> p c i j", j=WIN_COLS),
                 in0=window_of(q_bands[win // SPLIT][:], win % SPLIT),
                 scalar1=CK**-0.5,
-                scalar2=None,
+                scalar2=0.0,
                 op0=MULT,
+                op1=ADD,
             )
             tiles[("q", win)] = q_win
 
-        def x_scalar(win, part):
-            if part == 0:
-                tiles[("x", win)] = work.tile([P, TOKENS, PACK], BF16, name="x_grouped", align_bytes=64)
-            first = VECTOR_ROWS + part * SCALAR_ROWS
-            x_win = window_of(x_bands[win // SPLIT][:], win % SPLIT)
-            nc.scalar.copy(
-                out=tiles[("x", win)][:, first * WIN_COLS : (first + SCALAR_ROWS) * WIN_COLS, :].rearrange(
-                    "p (i j) c -> p i j c", j=WIN_COLS
-                ),
-                in_=x_win[:, :, first : first + SCALAR_ROWS, :].rearrange("p c i j -> p i j c"),
+        def x_group(win):
+            x_grouped = x_pool.tile([P, TOKENS, PACK], BF16, align_bytes=64)
+            nc.gpsimd.tensor_scalar(
+                out=x_grouped[:].rearrange("p (i j) c -> p i j c", j=WIN_COLS),
+                in0=window_of(x_bands[win // SPLIT][:], win % SPLIT).rearrange("p c i j -> p i j c"),
+                scalar1=1.0,
+                scalar2=0.0,
+                op0=MULT,
+                op1=ADD,
             )
-
-        def x_vector(win):
-            x_win = window_of(x_bands[win // SPLIT][:], win % SPLIT)
-            nc.vector.tensor_copy(
-                out=tiles[("x", win)][:, : VECTOR_ROWS * WIN_COLS, :].rearrange(
-                    "p (i g r) c -> p i g c r", g=WIN_COLS // RUN, r=RUN
-                ),
-                in_=x_win[:, :, :VECTOR_ROWS, :].rearrange("p c i (g r) -> p i g c r", r=RUN),
-            )
+            tiles[("x", win)] = x_grouped
 
         def x_quantise(win):
             x_codes = work.tile([P, TOKENS], U32, align_bytes=64)
@@ -285,13 +276,12 @@ def tile_pyramidselfattentionblock_pa_kernel(tc, x, q, k, v_w, v_b, out):
             if 0 <= win < N_WINDOWS:
                 stage(win, *args)
 
-        for c in range(-2, N_WINDOWS + 2):
+        for c in range(-3, N_WINDOWS + 2):
             run(sim_matmul, c, 1)
             run(ctx_matmul, c - 2, 0)
             run(ctx_matmul, c - 2, 1)
+            run(v_matmul, c - 1, 0)
             run(row_max, c, 0)
-            run(v_bias, c, 1)
-            run(q_window, c + 1)
             run(exponent, c - 1, 3)
             run(inv_copy, c - 2)
             run(e_copy, c - 1, 0)
@@ -300,18 +290,13 @@ def tile_pyramidselfattentionblock_pa_kernel(tc, x, q, k, v_w, v_b, out):
             run(e_turn, c - 1, 1)
             run(row_max, c, 1)
             run(ctx_scale, c - 2, 0)
-            run(x_quantise, c + 1)
             run(exponent, c, 0)
-            run(x_scalar, c + 2, 0)
 
             run(sim_matmul, c, 3)
-            run(v_matmul, c + 1, 0)
-            run(v_matmul, c + 1, 1)
+            run(v_matmul, c - 1, 1)
             run(row_max, c, 2)
             run(ctx_scale, c - 2, 1)
-            run(v_quantise, c)
             run(sum_invert, c - 1)
-            run(x_vector, c + 2)
             run(exponent, c, 1)
             run(e_copy, c - 1, 1)
 
@@ -319,7 +304,11 @@ def tile_pyramidselfattentionblock_pa_kernel(tc, x, q, k, v_w, v_b, out):
             run(e_turn, c, 0)
             run(inv_turn, c - 1)
             run(row_max, c, 3)
+            run(v_bias, c - 1, 0)
+            run(v_bias, c - 1, 1)
             run(e_quantise, c - 1)
-            run(v_bias, c + 1, 0)
+            run(v_quantise, c - 1)
+            run(x_quantise, c)
             run(exponent, c, 2)
-            run(x_scalar, c + 2, 1)
+            run(x_group, c + 1)
+            run(q_window, c + 3)

@@ -57,7 +57,6 @@ def tile_pyramidselfattentionblock_pa_kernel(tc, x, q, k, v_w, v_b, out):
             in_=v_w.rearrange("(h p) c -> p h c", p=P),
         )
         bias = const.tile([P, CV], BF16)
-        nc.sync.dma_start(out=bias[:], in_=v_b.partition_broadcast(P))
         q_bands, k_bands, x_bands = [], [], []
         for band in range(N_BANDS):
             image, pixels = band // SPLIT, slice((band % SPLIT) * BAND, (band % SPLIT + 1) * BAND)
@@ -70,6 +69,8 @@ def tile_pyramidselfattentionblock_pa_kernel(tc, x, q, k, v_w, v_b, out):
             q_bands.append(q_raw)
             k_bands.append(k_raw)
             x_bands.append(x_raw)
+            if band == 0:
+                nc.sync.dma_start(out=bias[:], in_=v_b.partition_broadcast(P))
 
         ident_f32 = const.tile([P, P], F32)
         make_identity(nc, ident_f32[:])

@@ -74,8 +74,6 @@ def tile_pyramidselfattentionblock_pa_kernel(tc, x, q, k, v_w, v_b, out):
 
         ident_f32 = const.tile([P, P], F32)
         make_identity(nc, ident_f32[:])
-        ident_bf16 = const.tile([P, P], BF16)
-        make_identity(nc, ident_bf16[:])
 
         w_words = w_raw[:].bitcast(F32).rearrange("p (h w u) -> p h u w", h=CV_TILES, u=2)
         w_turned = turn_banks.tile([P, 2, CV], F32, tag="turn")
@@ -185,8 +183,8 @@ def tile_pyramidselfattentionblock_pa_kernel(tc, x, q, k, v_w, v_b, out):
                 tiles[("sum", win)] = work.tile([P, ROW_TILES], F32, name="row_sum")
             e_rows = rows.tile([P, TOKENS], BF16)
             nc.scalar.activation(
-                out=e_rows[:],
-                in_=tiles[("sim", win, r)][:],
+                out=e_rows[:].rearrange("p (u k e) -> p u k e", u=2, e=2),
+                in_=tiles[("sim", win, r)][:].rearrange("p (u e k) -> p u k e", u=2, e=2),
                 func=EXP,
                 bias=tiles[("max", win)][:, r : r + 1],
                 scale=1.0,
@@ -195,22 +193,24 @@ def tile_pyramidselfattentionblock_pa_kernel(tc, x, q, k, v_w, v_b, out):
             tiles[("e", win, r)] = e_rows
 
         def e_turn(win, half):
-            e_turned = turn_banks.tile([P, PACK, HALF], BF16, tag="turn")
+            e_turned = turn_banks.tile([P, 2, HALF], F32, tag="turn")
             for r in range(HALF // P):
-                for t in range(PACK):
+                e_words = tiles[("e", win, half * (HALF // P) + r)][:].bitcast(F32)
+                for u in range(2):
                     nc.tensor.transpose(
-                        out=e_turned[:, t, r * P : (r + 1) * P],
-                        in_=tiles[("e", win, half * (HALF // P) + r)][:, t * P : (t + 1) * P],
-                        identity=ident_bf16[:],
+                        out=e_turned[:, u, r * P : (r + 1) * P],
+                        in_=e_words[:, u * P : (u + 1) * P],
+                        identity=ident_f32[:],
                     )
             tiles[("et", win, half)] = e_turned
 
         def e_copy(win, half):
             if half == 0:
                 tiles[("eg", win)] = work.tile([P, TOKENS, PACK], BF16, name="e_grouped", align_bytes=64)
+            e_grouped = tiles[("eg", win)][:].rearrange("p l t -> p (l t)").bitcast(F32).rearrange("p (l u) -> p l u", u=2)
             nc.scalar.copy(
-                out=tiles[("eg", win)][:, half * HALF : (half + 1) * HALF, :],
-                in_=tiles[("et", win, half)][:].rearrange("p t l -> p l t"),
+                out=e_grouped[:, half * HALF : (half + 1) * HALF, :],
+                in_=tiles[("et", win, half)][:].rearrange("p u l -> p l u"),
             )
 
         def e_quantise(win):

@@ -51,68 +51,105 @@ def tile_pyramidselfattentionblock_pa_kernel(tc, x, q, k, v_w, v_b, out):
         turn_banks = ctx.enter_context(tc.psum_pool(name="turn_banks", bufs=2))
         mx_banks = ctx.enter_context(tc.psum_pool(name="mx_banks", bufs=3))
 
-        w_raw = const.tile([P, CV_TILES * CIN], BF16)
-        nc.sync.dma_start(
-            out=w_raw[:].rearrange("p (h c) -> p h c", h=CV_TILES),
-            in_=v_w.rearrange("(h p) c -> p h c", p=P),
-        )
-        bias = const.tile([P, CV], BF16)
+        w_raw = const.tile([P, CV_TILES, CIN], BF16)
+        bias_row = const.tile([P, CV], BF16)
+        nc.gpsimd.memset(bias_row[:], 0.0)
+        ones = const.tile([P, P], BF16)
+        nc.gpsimd.memset(ones[:], 1.0)
         q_bands, k_bands, x_bands = [], [], []
         for band in range(N_BANDS):
             image, pixels = band // SPLIT, slice((band % SPLIT) * BAND, (band % SPLIT + 1) * BAND)
+            q_map = q[image].rearrange("(c p) h w -> p c (h w)", p=P)[:, :, pixels]
+            k_map = k[image].rearrange("(c p) h w -> p c (h w)", p=P)[:, :, pixels]
+            x_map = x[image].rearrange("(p j) h w -> p j (h w)", j=PACK)[:, :, pixels]
             q_raw = maps.tile([P, CK_TILES, BAND], BF16)
-            nc.sync.dma_start(out=q_raw[:], in_=q[image].rearrange("(c p) h w -> p c (h w)", p=P)[:, :, pixels])
             k_raw = maps.tile([P, CK_TILES, BAND], BF16)
-            nc.sync.dma_start(out=k_raw[:], in_=k[image].rearrange("(c p) h w -> p c (h w)", p=P)[:, :, pixels])
             x_raw = maps.tile([P, PACK, BAND], BF16)
-            nc.sync.dma_start(out=x_raw[:], in_=x[image].rearrange("(p j) h w -> p j (h w)", j=PACK)[:, :, pixels])
+            if band == 0:
+                first, rest = slice(0, BAND // ROW_TILES), slice(BAND // ROW_TILES, BAND)
+                nc.sync.dma_start(out=q_raw[:, :, first], in_=q_map[:, :, first])
+                nc.sync.dma_start(out=k_raw[:], in_=k_map)
+                nc.sync.dma_start(out=q_raw[:, :, rest], in_=q_map[:, :, rest])
+                for rows_half in (slice(0, BAND // 2), slice(BAND // 2, BAND)):
+                    nc.sync.dma_start(out=x_raw[:, :, rows_half], in_=x_map[:, :, rows_half])
+                nc.sync.dma_start(out=w_raw[:], in_=v_w.rearrange("(h p) c -> p h c", p=P))
+                nc.sync.dma_start(out=bias_row[0:1, :], in_=v_b.rearrange("(u o) -> u o", u=1))
+            else:
+                nc.sync.dma_start(out=q_raw[:], in_=q_map)
+                nc.sync.dma_start(out=k_raw[:], in_=k_map)
+                nc.sync.dma_start(out=x_raw[:], in_=x_map)
             q_bands.append(q_raw)
             k_bands.append(k_raw)
             x_bands.append(x_raw)
-            if band == 0:
-                nc.sync.dma_start(out=bias[:], in_=v_b.partition_broadcast(P))
 
         ident_f32 = const.tile([P, P], F32)
         make_identity(nc, ident_f32[:])
 
-        w_words = w_raw[:].bitcast(F32).rearrange("p (h w u) -> p h u w", h=CV_TILES, u=2)
-        w_turned = turn_banks.tile([P, 2, CV], F32, tag="turn")
-        for h in range(CV_TILES):
-            for u in range(2):
-                nc.tensor.transpose(out=w_turned[:, u, h * P : (h + 1) * P], in_=w_words[:, h, u, :], identity=ident_f32[:])
-        w_grouped = const.tile([P, CV * PACK], BF16, align_bytes=64)
-        nc.vector.tensor_copy(
-            out=w_grouped[:].bitcast(F32).rearrange("p (o u) -> p o u", u=2),
-            in_=w_turned[:].rearrange("p u o -> p o u"),
-        )
-        w_codes = const.tile([P, CV], U32, align_bytes=64)
-        w_scales = const.tile([P, CV], U8, align_bytes=64)
-        nc.vector.quantize_mx(out=w_codes[:].bitcast(FP8X4), scales=w_scales[:], in_=w_grouped[:])
-
         tiles = {}
 
-        def q_window(win):
-            q_win = q_pool.tile([P, CK_TILES, TOKENS], BF16)
-            nc.gpsimd.tensor_scalar(
-                out=q_win[:].rearrange("p c (i j) -> p c i j", j=WIN_COLS),
-                in0=window_of(q_bands[win // SPLIT][:], win % SPLIT),
+        def w_turn():
+            w_words = w_raw[:].bitcast(F32).rearrange("p h (w u) -> p h u w", u=2)
+            w_turned = turn_banks.tile([P, 2, CV], F32, tag="turn")
+            for h in range(CV_TILES):
+                for u in range(2):
+                    nc.tensor.transpose(out=w_turned[:, u, h * P : (h + 1) * P], in_=w_words[:, h, u, :], identity=ident_f32[:])
+            tiles["wt"] = w_turned
+
+        def w_copy():
+            w_grouped = const.tile([P, CV * PACK], BF16, align_bytes=64)
+            nc.vector.tensor_copy(
+                out=w_grouped[:].bitcast(F32).rearrange("p (o u) -> p o u", u=2),
+                in_=tiles["wt"][:].rearrange("p u o -> p o u"),
+            )
+            tiles["wg"] = w_grouped
+
+        def w_quantise():
+            w_codes = const.tile([P, CV], U32, align_bytes=64)
+            w_scales = const.tile([P, CV], U8, align_bytes=64)
+            nc.vector.quantize_mx(out=w_codes[:].bitcast(FP8X4), scales=w_scales[:], in_=tiles["wg"][:])
+            tiles["wq"] = (w_codes, w_scales)
+
+        def bias_spread():
+            bias_acc = turn_banks.tile([P, CV], F32, tag="turn")
+            nc.tensor.matmul(out=bias_acc[:], lhsT=ones[:], rhs=bias_row[:], start=True, stop=True)
+            tiles["bacc"] = bias_acc
+
+        def bias_copy():
+            bias = const.tile([P, CV], F32)
+            nc.scalar.copy(out=bias[:], in_=tiles["bacc"][:])
+            tiles["bias"] = bias
+
+        def q_rows(win, top, bottom):
+            if top == 0:
+                tiles[("q", win)] = q_pool.tile([P, CK_TILES, TOKENS], BF16, name="q_win")
+            engine = nc.vector if win < 2 else nc.gpsimd
+            engine.tensor_scalar(
+                out=tiles[("q", win)][:].rearrange("p c (i j) -> p c i j", j=WIN_COLS)[:, :, top:bottom],
+                in0=window_of(q_bands[win // SPLIT][:], win % SPLIT)[:, :, top:bottom],
                 scalar1=CK**-0.5,
                 scalar2=0.0,
                 op0=MULT,
                 op1=ADD,
             )
-            tiles[("q", win)] = q_win
+
+        def q_window(win):
+            q_rows(win, 0, WIN_ROWS)
 
         def x_group(win):
             x_grouped = x_pool.tile([P, TOKENS, PACK], BF16, align_bytes=64)
+            grouped = x_grouped[:].rearrange("p (i j) c -> p i j c", j=WIN_COLS)
+            raw = window_of(x_bands[win // SPLIT][:], win % SPLIT).rearrange("p c i j -> p i j c")
+            gpsimd_rows = WIN_ROWS // 2 if win == 0 else WIN_ROWS
             nc.gpsimd.tensor_scalar(
-                out=x_grouped[:].rearrange("p (i j) c -> p i j c", j=WIN_COLS),
-                in0=window_of(x_bands[win // SPLIT][:], win % SPLIT).rearrange("p c i j -> p i j c"),
+                out=grouped[:, :gpsimd_rows],
+                in0=raw[:, :gpsimd_rows],
                 scalar1=1.0,
                 scalar2=0.0,
                 op0=MULT,
                 op1=ADD,
             )
+            if gpsimd_rows < WIN_ROWS:
+                nc.scalar.copy(out=grouped[:, gpsimd_rows:], in_=raw[:, gpsimd_rows:])
             tiles[("x", win)] = x_grouped
 
         def x_quantise(win):
@@ -125,6 +162,7 @@ def tile_pyramidselfattentionblock_pa_kernel(tc, x, q, k, v_w, v_b, out):
 
         def v_matmul(win, h):
             x_codes, x_scales = tiles[("xq", win)]
+            w_codes, w_scales = tiles["wq"]
             channels = slice(h * P, (h + 1) * P)
             v_acc = mx_banks.tile([P, PACK, P], F32, tag="mx")
             for t in range(PACK):
@@ -146,7 +184,7 @@ def tile_pyramidselfattentionblock_pa_kernel(tc, x, q, k, v_w, v_b, out):
             nc.vector.tensor_tensor(
                 out=tiles[("vg", win)][:, h],
                 in0=tiles[("vacc", win, h)][:].rearrange("p t o -> p o t"),
-                in1=bias[:, h * P : (h + 1) * P].unsqueeze(2).to_broadcast([P, P, PACK]),
+                in1=tiles["bias"][:, h * P : (h + 1) * P].unsqueeze(2).to_broadcast([P, P, PACK]),
                 op=ADD,
             )
 
@@ -277,12 +315,16 @@ def tile_pyramidselfattentionblock_pa_kernel(tc, x, q, k, v_w, v_b, out):
             if 0 <= win < N_WINDOWS:
                 stage(win, *args)
 
-        for c in range(-3, N_WINDOWS + 2):
+        q_rows(0, 0, WIN_ROWS // ROW_TILES)
+        q_rows(0, WIN_ROWS // ROW_TILES, WIN_ROWS)
+        for c in range(-1, N_WINDOWS + 2):
             run(sim_matmul, c, 1)
             run(ctx_matmul, c - 2, 0)
             run(ctx_matmul, c - 2, 1)
             run(v_matmul, c - 1, 0)
             run(row_max, c, 0)
+            if c == 0:
+                q_window(1)
             run(exponent, c - 1, 3)
             run(inv_copy, c - 2)
             run(e_copy, c - 1, 0)
@@ -300,16 +342,27 @@ def tile_pyramidselfattentionblock_pa_kernel(tc, x, q, k, v_w, v_b, out):
             run(sum_invert, c - 1)
             run(exponent, c, 1)
             run(e_copy, c - 1, 1)
+            if c == 0:
+                x_group(0)
+                w_turn()
+                bias_spread()
 
             run(sim_matmul, c + 1, 0)
             run(e_turn, c, 0)
             run(inv_turn, c - 1)
             run(row_max, c, 3)
+            if c == 0:
+                w_copy()
+                w_quantise()
             run(v_bias, c - 1, 0)
             run(v_bias, c - 1, 1)
             run(e_quantise, c - 1)
             run(v_quantise, c - 1)
             run(x_quantise, c)
             run(exponent, c, 2)
-            run(x_group, c + 1)
-            run(q_window, c + 3)
+            if c == 0:
+                bias_copy()
+                q_window(2)
+            if c >= 0:
+                run(x_group, c + 1)
+                run(q_window, c + 3)

@@ -11,6 +11,7 @@ FP8X4 = mybir.dt.float8_e4m3fn_x4
 ADD = mybir.AluOpType.add
 MULT = mybir.AluOpType.mult
 MAX = mybir.AluOpType.max
+IDENTITY = mybir.ActivationFunctionType.Identity
 EXP = mybir.ActivationFunctionType.Exp
 FREE_AXIS = mybir.AxisListType.X
 
@@ -26,6 +27,8 @@ N_WINDOWS = N_BANDS * SPLIT
 CK_TILES = CK // P
 CV_TILES = CV // P
 ROW_TILES = TOKENS // P
+BIAS_COLS = 4
+ALL = slice(0, TOKENS)
 HALF = TOKENS // 2
 
 FLOPS = 2 * IMAGES * CV * CIN * SPLIT * BAND + 2 * 2 * N_WINDOWS * TOKENS * TOKENS * CK
@@ -110,12 +113,13 @@ def tile_pyramidselfattentionblock_pa_kernel(tc, x, q, k, v_w, v_b, out):
             tiles["wq"] = (w_codes, w_scales)
 
         def bias_spread():
-            bias_acc = turn_banks.tile([P, CV], F32, tag="turn")
-            nc.tensor.matmul(out=bias_acc[:], lhsT=ones[:], rhs=bias_row[:], start=True, stop=True)
+            bias_acc = turn_banks.tile([P, P + BIAS_COLS], F32, tag="turn")
+            nc.tensor.matmul(out=bias_acc[:, :P], lhsT=ones[:], rhs=bias_row[:, :P], start=True, stop=True)
+            nc.tensor.matmul(out=bias_acc[:, P:], lhsT=bias_row[:, P:], rhs=ones[:, :BIAS_COLS], start=True, stop=True)
             tiles["bacc"] = bias_acc
 
         def bias_copy():
-            bias = const.tile([P, CV], F32)
+            bias = const.tile([P, P + BIAS_COLS], F32)
             nc.scalar.copy(out=bias[:], in_=tiles["bacc"][:])
             tiles["bias"] = bias
 
@@ -160,10 +164,9 @@ def tile_pyramidselfattentionblock_pa_kernel(tc, x, q, k, v_w, v_b, out):
             )
             tiles[("xq", win)] = (x_codes, x_scales)
 
-        def v_matmul(win, h):
+        def v_matmul_keys(win):
             x_codes, x_scales = tiles[("xq", win)]
             w_codes, w_scales = tiles["wq"]
-            channels = slice(h * P, (h + 1) * P)
             v_acc = mx_banks.tile([P, PACK, P], F32, tag="mx")
             for t in range(PACK):
                 keys = slice(t * P, (t + 1) * P)
@@ -171,28 +174,64 @@ def tile_pyramidselfattentionblock_pa_kernel(tc, x, q, k, v_w, v_b, out):
                     out=v_acc[:, t, :],
                     lhsT=x_codes[:, keys].bitcast(FP8X4),
                     lhsT_scale=x_scales[:, keys],
-                    rhs=w_codes[:, channels].bitcast(FP8X4),
-                    rhs_scale=w_scales[:, channels],
+                    rhs=w_codes[:, :P].bitcast(FP8X4),
+                    rhs_scale=w_scales[:, :P],
                     start=True,
                     stop=True,
                 )
-            tiles[("vacc", win, h)] = v_acc
+            tiles[("vacc", win, 0)] = v_acc
+            tiles[("vg", win)] = work.tile([P, CV, PACK], BF16, name="v_grouped", align_bytes=64)
 
-        def v_bias(win, h):
-            if h == 0:
-                tiles[("vg", win)] = work.tile([P, CV_TILES, P, PACK], BF16, name="v_grouped", align_bytes=64)
+        def v_bias_keys(win):
             nc.vector.tensor_tensor(
-                out=tiles[("vg", win)][:, h],
-                in0=tiles[("vacc", win, h)][:].rearrange("p t o -> p o t"),
-                in1=tiles["bias"][:, h * P : (h + 1) * P].unsqueeze(2).to_broadcast([P, P, PACK]),
+                out=tiles[("vg", win)][:, :P],
+                in0=tiles[("vacc", win, 0)][:].rearrange("p t o -> p o t"),
+                in1=tiles["bias"][:, :P].unsqueeze(2).to_broadcast([P, P, PACK]),
                 op=ADD,
             )
+
+        def v_matmul_channels(win):
+            x_codes, x_scales = tiles[("xq", win)]
+            w_codes, w_scales = tiles["wq"]
+            v_acc = mx_banks.tile([P, TOKENS], F32, tag="mx")
+            nc.tensor.matmul_mx(
+                out=v_acc[:],
+                lhsT=w_codes[:, P:].bitcast(FP8X4),
+                lhsT_scale=w_scales[:, P:],
+                rhs=x_codes[:].bitcast(FP8X4),
+                rhs_scale=x_scales[:],
+                start=True,
+                stop=True,
+            )
+            tiles[("vacc", win, 1)] = v_acc
+
+        def v_bias_channels(win):
+            v_rows = rows.tile([P, TOKENS], BF16)
+            nc.scalar.activation(
+                out=v_rows[:].rearrange("p (u k e) -> p u k e", u=2, e=2),
+                in_=tiles[("vacc", win, 1)][:].rearrange("p (u e k) -> p u k e", u=2, e=2),
+                func=IDENTITY,
+                bias=tiles["bias"][:, P : P + 1],
+                scale=1.0,
+            )
+            tiles[("v", win)] = v_rows
+
+        def v_turn(win):
+            v_turned = turn_banks.tile([P, 2, P], F32, tag="turn")
+            v_words = tiles[("v", win)][:].bitcast(F32)
+            for u in range(2):
+                nc.tensor.transpose(out=v_turned[:, u, :], in_=v_words[:, u * P : (u + 1) * P], identity=ident_f32[:])
+            tiles[("vt", win)] = v_turned
+
+        def v_copy(win):
+            words = tiles[("vg", win)][:].rearrange("p o t -> p (o t)").bitcast(F32).rearrange("p (o u) -> p o u", u=2)
+            nc.scalar.copy(out=words[:, P:], in_=tiles[("vt", win)][:].rearrange("p u o -> p o u"))
 
         def v_quantise(win):
             v_codes = work.tile([P, CV], U32, align_bytes=64)
             v_scales = work.tile([P, CV], U8, align_bytes=64)
             nc.vector.quantize_mx(
-                out=v_codes[:].bitcast(FP8X4), scales=v_scales[:], in_=tiles[("vg", win)][:].rearrange("p h o t -> p (h o t)")
+                out=v_codes[:].bitcast(FP8X4), scales=v_scales[:], in_=tiles[("vg", win)][:].rearrange("p o t -> p (o t)")
             )
             tiles[("vq", win)] = (v_codes, v_scales)
 
@@ -251,13 +290,18 @@ def tile_pyramidselfattentionblock_pa_kernel(tc, x, q, k, v_w, v_b, out):
                 in_=tiles[("et", win, half)][:].rearrange("p u l -> p l u"),
             )
 
-        def e_quantise(win):
-            e_codes = work.tile([P, TOKENS], U32, align_bytes=64)
-            e_scales = work.tile([P, TOKENS], U8, align_bytes=64)
+        def e_quantise(win, part=ALL):
+            if part.start == 0:
+                tiles[("eq", win)] = (
+                    work.tile([P, TOKENS], U32, name="e_codes", align_bytes=64),
+                    work.tile([P, TOKENS], U8, name="e_scales", align_bytes=64),
+                )
+            e_codes, e_scales = tiles[("eq", win)]
             nc.vector.quantize_mx(
-                out=e_codes[:].bitcast(FP8X4), scales=e_scales[:], in_=tiles[("eg", win)][:].rearrange("p l t -> p (l t)")
+                out=e_codes[:, part].bitcast(FP8X4),
+                scales=e_scales[:, part],
+                in_=tiles[("eg", win)][:, part].rearrange("p l t -> p (l t)"),
             )
-            tiles[("eq", win)] = (e_codes, e_scales)
 
         def sum_invert(win):
             inv_sum = work.tile([P, ROW_TILES], F32)
@@ -279,36 +323,37 @@ def tile_pyramidselfattentionblock_pa_kernel(tc, x, q, k, v_w, v_b, out):
             nc.scalar.copy(out=inv_all[:], in_=tiles[("invt", win)][:])
             tiles[("inva", win)] = inv_all
 
-        def ctx_matmul(win, h):
+        def ctx_matmul(win, h, part=ALL):
             v_codes, v_scales = tiles[("vq", win)]
             e_codes, e_scales = tiles[("eq", win)]
-            ctx_acc = mx_banks.tile([P, TOKENS], F32, tag="mx")
+            if part.start == 0:
+                tiles[("ctx", win, h)] = mx_banks.tile([P, TOKENS], F32, name="ctx_acc", tag="mx")
             nc.tensor.matmul_mx(
-                out=ctx_acc[:],
+                out=tiles[("ctx", win, h)][:, part],
                 lhsT=v_codes[:, h * P : (h + 1) * P].bitcast(FP8X4),
                 lhsT_scale=v_scales[:, h * P : (h + 1) * P],
-                rhs=e_codes[:].bitcast(FP8X4),
-                rhs_scale=e_scales[:],
+                rhs=e_codes[:, part].bitcast(FP8X4),
+                rhs_scale=e_scales[:, part],
                 start=True,
                 stop=True,
             )
-            tiles[("ctx", win, h)] = ctx_acc
 
-        def ctx_scale(win, h):
+        def ctx_scale(win, h, part=ALL):
             band, side = win // SPLIT, win % SPLIT
             if side == 0:
                 tiles[("out", band, h)] = work.tile([P, BAND], F32, name="out_band%d" % h)
+            top, bottom = part.start // WIN_COLS, part.stop // WIN_COLS
             nc.vector.tensor_tensor(
-                out=window_of(tiles[("out", band, h)][:], side),
-                in0=tiles[("ctx", win, h)][:].rearrange("p (i j) -> p i j", j=WIN_COLS),
-                in1=tiles[("inva", win)][:].rearrange("p (i j) -> p i j", j=WIN_COLS),
+                out=window_of(tiles[("out", band, h)][:], side)[:, top:bottom],
+                in0=tiles[("ctx", win, h)][:, part].rearrange("p (i j) -> p i j", j=WIN_COLS),
+                in1=tiles[("inva", win)][:, part].rearrange("p (i j) -> p i j", j=WIN_COLS),
                 op=MULT,
             )
             if side == SPLIT - 1:
                 image, first_row = band // SPLIT, (band % SPLIT) * WIN_ROWS
                 nc.sync.dma_start(
-                    out=out[image, h * P : (h + 1) * P, first_row : first_row + WIN_ROWS, :].rearrange("o h w -> o (h w)"),
-                    in_=tiles[("out", band, h)][:],
+                    out=out[image, h * P : (h + 1) * P, first_row + top : first_row + bottom, :].rearrange("o h w -> o (h w)"),
+                    in_=tiles[("out", band, h)][:, SPLIT * part.start : SPLIT * part.stop],
                 )
 
         def run(stage, win, *args):
@@ -317,26 +362,29 @@ def tile_pyramidselfattentionblock_pa_kernel(tc, x, q, k, v_w, v_b, out):
 
         q_rows(0, 0, WIN_ROWS // ROW_TILES)
         q_rows(0, WIN_ROWS // ROW_TILES, WIN_ROWS)
-        for c in range(-1, N_WINDOWS + 2):
+        last = N_WINDOWS - 1
+        for c in range(-1, N_WINDOWS):
             run(sim_matmul, c, 1)
             run(ctx_matmul, c - 2, 0)
             run(ctx_matmul, c - 2, 1)
-            run(v_matmul, c - 1, 0)
+            run(v_matmul_channels, c - 1)
             run(row_max, c, 0)
             if c == 0:
                 q_window(1)
             run(exponent, c - 1, 3)
-            run(inv_copy, c - 2)
             run(e_copy, c - 1, 0)
+            run(inv_copy, c - 2)
 
             run(sim_matmul, c, 2)
             run(e_turn, c - 1, 1)
             run(row_max, c, 1)
             run(ctx_scale, c - 2, 0)
             run(exponent, c, 0)
+            run(v_bias_channels, c - 1)
 
             run(sim_matmul, c, 3)
-            run(v_matmul, c - 1, 1)
+            run(v_matmul_keys, c - 1)
+            run(v_turn, c - 1)
             run(row_max, c, 2)
             run(ctx_scale, c - 2, 1)
             run(sum_invert, c - 1)
@@ -354,15 +402,45 @@ def tile_pyramidselfattentionblock_pa_kernel(tc, x, q, k, v_w, v_b, out):
             if c == 0:
                 w_copy()
                 w_quantise()
-            run(v_bias, c - 1, 0)
-            run(v_bias, c - 1, 1)
+            run(exponent, c, 2)
+            run(v_copy, c - 1)
+            if c == last:
+                x_quantise(last)
+            run(v_bias_keys, c - 1)
             run(e_quantise, c - 1)
             run(v_quantise, c - 1)
-            run(x_quantise, c)
-            run(exponent, c, 2)
+            if c < last:
+                run(x_quantise, c)
             if c == 0:
                 bias_copy()
                 q_window(2)
             if c >= 0:
                 run(x_group, c + 1)
                 run(q_window, c + 3)
+
+        v_matmul_channels(last)
+        v_matmul_keys(last)
+        ctx_matmul(last - 1, 0)
+        ctx_matmul(last - 1, 1)
+        exponent(last, 3)
+        v_bias_channels(last)
+        sum_invert(last)
+        v_bias_keys(last)
+        inv_copy(last - 1)
+        ctx_scale(last - 1, 0)
+        v_turn(last)
+        e_turn(last, 1)
+        inv_turn(last)
+        ctx_scale(last - 1, 1)
+        e_copy(last, 0)
+        v_copy(last)
+        e_copy(last, 1)
+        inv_copy(last)
+        v_quantise(last)
+        halves = (slice(0, HALF), slice(HALF, TOKENS))
+        for part in halves:
+            e_quantise(last, part)
+        for part in halves:
+            for h in range(CV_TILES):
+                ctx_matmul(last, h, part)
+                ctx_scale(last, h, part)

@@ -28,6 +28,8 @@ CK_TILES = CK // P
 CV_TILES = CV // P
 ROW_TILES = TOKENS // P
 BIAS_COLS = 4
+GPSIMD_ROWS = 14
+WARM_UPS = 6
 ALL = slice(0, TOKENS)
 HALF = TOKENS // 2
 
@@ -57,6 +59,8 @@ def tile_pyramidselfattentionblock_pa_kernel(tc, x, q, k, v_w, v_b, out):
         w_raw = const.tile([P, CV_TILES, CIN], BF16)
         bias_row = const.tile([P, CV], BF16)
         nc.gpsimd.memset(bias_row[:], 0.0)
+        zeros = const.tile([P, TOKENS], BF16)
+        nc.vector.memset(zeros[:], 0.0)
         ones = const.tile([P, P], BF16)
         nc.gpsimd.memset(ones[:], 1.0)
         q_bands, k_bands, x_bands = [], [], []
@@ -84,6 +88,10 @@ def tile_pyramidselfattentionblock_pa_kernel(tc, x, q, k, v_w, v_b, out):
             q_bands.append(q_raw)
             k_bands.append(k_raw)
             x_bands.append(x_raw)
+
+        for w in range(WARM_UPS):
+            warm = turn_banks.tile([P, TOKENS], F32, tag="turn")
+            nc.tensor.matmul(out=warm[:], lhsT=zeros[:, :P], rhs=zeros[:], start=True, stop=True)
 
         ident_f32 = const.tile([P, P], F32)
         make_identity(nc, ident_f32[:])
@@ -139,22 +147,23 @@ def tile_pyramidselfattentionblock_pa_kernel(tc, x, q, k, v_w, v_b, out):
         def q_window(win):
             q_rows(win, 0, WIN_ROWS)
 
-        def x_group(win):
-            x_grouped = x_pool.tile([P, TOKENS, PACK], BF16, align_bytes=64)
-            grouped = x_grouped[:].rearrange("p (i j) c -> p i j c", j=WIN_COLS)
-            raw = window_of(x_bands[win // SPLIT][:], win % SPLIT).rearrange("p c i j -> p i j c")
-            gpsimd_rows = WIN_ROWS // 2 if win == 0 else WIN_ROWS
-            nc.gpsimd.tensor_scalar(
-                out=grouped[:, :gpsimd_rows],
-                in0=raw[:, :gpsimd_rows],
-                scalar1=1.0,
-                scalar2=0.0,
-                op0=MULT,
-                op1=ADD,
-            )
-            if gpsimd_rows < WIN_ROWS:
-                nc.scalar.copy(out=grouped[:, gpsimd_rows:], in_=raw[:, gpsimd_rows:])
-            tiles[("x", win)] = x_grouped
+        def x_rows(engine, win, top, bottom):
+            if top == 0:
+                tiles[("x", win)] = x_pool.tile([P, TOKENS, PACK], BF16, name="x_grouped", align_bytes=64)
+            grouped = tiles[("x", win)][:].rearrange("p (i j) c -> p i j c", j=WIN_COLS)[:, top:bottom]
+            raw = window_of(x_bands[win // SPLIT][:], win % SPLIT).rearrange("p c i j -> p i j c")[:, top:bottom]
+            if engine == nc.scalar:
+                nc.scalar.copy(out=grouped, in_=raw)
+            elif engine == nc.vector:
+                nc.vector.tensor_copy(out=grouped, in_=raw)
+            else:
+                nc.gpsimd.tensor_scalar(out=grouped, in0=raw, scalar1=1.0, scalar2=0.0, op0=MULT, op1=ADD)
+
+        def x_gpsimd(win):
+            x_rows(nc.gpsimd, win, 0, GPSIMD_ROWS)
+
+        def x_scalar(win):
+            x_rows(nc.scalar, win, GPSIMD_ROWS, WIN_ROWS)
 
         def x_quantise(win):
             x_codes = work.tile([P, TOKENS], U32, align_bytes=64)
@@ -237,7 +246,7 @@ def tile_pyramidselfattentionblock_pa_kernel(tc, x, q, k, v_w, v_b, out):
 
         def sim_matmul(win, r):
             k_win = window_of(k_bands[win // SPLIT][:], win % SPLIT)
-            sim = sim_banks.tile([P, TOKENS], F32)
+            sim = sim_banks.tile([P, TOKENS], F32, tag="sim")
             for c in range(CK_TILES):
                 nc.tensor.matmul(
                     out=sim[:].rearrange("p (i j) -> p i j", j=WIN_COLS),
@@ -327,9 +336,12 @@ def tile_pyramidselfattentionblock_pa_kernel(tc, x, q, k, v_w, v_b, out):
             v_codes, v_scales = tiles[("vq", win)]
             e_codes, e_scales = tiles[("eq", win)]
             if part.start == 0:
-                tiles[("ctx", win, h)] = mx_banks.tile([P, TOKENS], F32, name="ctx_acc", tag="mx")
+                ctx_acc = mx_banks.tile([P, TOKENS], F32, tag="mx")
+            else:
+                ctx_acc = sim_banks.tile([P, TOKENS], F32, tag="sim")
+            tiles[("ctx", win, h, part.start)] = ctx_acc
             nc.tensor.matmul_mx(
-                out=tiles[("ctx", win, h)][:, part],
+                out=ctx_acc[:, part],
                 lhsT=v_codes[:, h * P : (h + 1) * P].bitcast(FP8X4),
                 lhsT_scale=v_scales[:, h * P : (h + 1) * P],
                 rhs=e_codes[:, part].bitcast(FP8X4),
@@ -345,7 +357,7 @@ def tile_pyramidselfattentionblock_pa_kernel(tc, x, q, k, v_w, v_b, out):
             top, bottom = part.start // WIN_COLS, part.stop // WIN_COLS
             nc.vector.tensor_tensor(
                 out=window_of(tiles[("out", band, h)][:], side)[:, top:bottom],
-                in0=tiles[("ctx", win, h)][:, part].rearrange("p (i j) -> p i j", j=WIN_COLS),
+                in0=tiles[("ctx", win, h, part.start)][:, part].rearrange("p (i j) -> p i j", j=WIN_COLS),
                 in1=tiles[("inva", win)][:, part].rearrange("p (i j) -> p i j", j=WIN_COLS),
                 op=MULT,
             )
@@ -379,6 +391,8 @@ def tile_pyramidselfattentionblock_pa_kernel(tc, x, q, k, v_w, v_b, out):
             run(e_turn, c - 1, 1)
             run(row_max, c, 1)
             run(ctx_scale, c - 2, 0)
+            if c > 1:
+                run(x_scalar, c)
             run(exponent, c, 0)
             run(v_bias_channels, c - 1)
 
@@ -391,7 +405,8 @@ def tile_pyramidselfattentionblock_pa_kernel(tc, x, q, k, v_w, v_b, out):
             run(exponent, c, 1)
             run(e_copy, c - 1, 1)
             if c == 0:
-                x_group(0)
+                x_rows(nc.gpsimd, 0, 0, 8)
+                x_rows(nc.scalar, 0, 8, 16)
                 w_turn()
                 bias_spread()
 
@@ -415,32 +430,38 @@ def tile_pyramidselfattentionblock_pa_kernel(tc, x, q, k, v_w, v_b, out):
                 bias_copy()
                 q_window(2)
             if c >= 0:
-                run(x_group, c + 1)
+                if c == 0:
+                    x_rows(nc.gpsimd, 1, 0, 16)
+                else:
+                    run(x_gpsimd, c + 1)
                 run(q_window, c + 3)
 
+        halves = (slice(0, HALF), slice(HALF, TOKENS))
         v_matmul_channels(last)
         v_matmul_keys(last)
-        ctx_matmul(last - 1, 0)
-        ctx_matmul(last - 1, 1)
         exponent(last, 3)
         v_bias_channels(last)
         sum_invert(last)
         v_bias_keys(last)
-        inv_copy(last - 1)
-        ctx_scale(last - 1, 0)
         v_turn(last)
+        ctx_matmul(last - 1, 0)
+        ctx_matmul(last - 1, 1)
+        inv_copy(last - 1)
+        v_copy(last)
+        ctx_scale(last - 1, 0)
         e_turn(last, 1)
         inv_turn(last)
-        ctx_scale(last - 1, 1)
         e_copy(last, 0)
-        v_copy(last)
         e_copy(last, 1)
         inv_copy(last)
         v_quantise(last)
-        halves = (slice(0, HALF), slice(HALF, TOKENS))
-        for part in halves:
-            e_quantise(last, part)
-        for part in halves:
-            for h in range(CV_TILES):
-                ctx_matmul(last, h, part)
-                ctx_scale(last, h, part)
+        e_quantise(last, halves[0])
+        ctx_scale(last - 1, 1)
+        for h in range(CV_TILES):
+            ctx_matmul(last, h, halves[0])
+        e_quantise(last, halves[1])
+        for h in range(CV_TILES):
+            ctx_scale(last, h, halves[0])
+            ctx_matmul(last, h, halves[1])
+        for h in range(CV_TILES):
+            ctx_scale(last, h, halves[1])

@@ -73,13 +73,12 @@ def tile_pyramidselfattentionblock_pa_kernel(tc, x, q, k, v_w, v_b, out):
             k_raw = maps.tile([P, CK_TILES, BAND], BF16)
             x_raw = maps.tile([P, PACK, BAND], BF16)
             if band == 0:
-                first, rest = slice(0, BAND // ROW_TILES), slice(BAND // ROW_TILES, BAND)
-                nc.sync.dma_start(out=q_raw[:, :, first], in_=q_map[:, :, first])
+                nc.sync.dma_start(out=q_raw[:], in_=q_map)
                 nc.sync.dma_start(out=k_raw[:], in_=k_map)
-                nc.sync.dma_start(out=q_raw[:, :, rest], in_=q_map[:, :, rest])
-                for rows_half in (slice(0, BAND // 2), slice(BAND // 2, BAND)):
-                    nc.sync.dma_start(out=x_raw[:, :, rows_half], in_=x_map[:, :, rows_half])
+                upper, lower = slice(0, BAND // 2), slice(BAND // 2, BAND)
+                nc.sync.dma_start(out=x_raw[:, :, upper], in_=x_map[:, :, upper])
                 nc.sync.dma_start(out=w_raw[:], in_=v_w.rearrange("(h p) c -> p h c", p=P))
+                nc.sync.dma_start(out=x_raw[:, :, lower], in_=x_map[:, :, lower])
                 nc.sync.dma_start(out=bias_row[0:1, :], in_=v_b.rearrange("(u o) -> u o", u=1))
             else:
                 nc.sync.dma_start(out=q_raw[:], in_=q_map)
@@ -225,8 +224,13 @@ def tile_pyramidselfattentionblock_pa_kernel(tc, x, q, k, v_w, v_b, out):
             )
             tiles[("v", win)] = v_rows
 
+        def turn_bank(win, shape):
+            if win == N_WINDOWS - 1:
+                return sim_banks.tile(shape, F32, name="turned", tag="sim")
+            return turn_banks.tile(shape, F32, name="turned", tag="turn")
+
         def v_turn(win):
-            v_turned = turn_banks.tile([P, 2, P], F32, tag="turn")
+            v_turned = turn_bank(win, [P, 2, P])
             v_words = tiles[("v", win)][:].bitcast(F32)
             for u in range(2):
                 nc.tensor.transpose(out=v_turned[:, u, :], in_=v_words[:, u * P : (u + 1) * P], identity=ident_f32[:])
@@ -246,7 +250,8 @@ def tile_pyramidselfattentionblock_pa_kernel(tc, x, q, k, v_w, v_b, out):
 
         def sim_matmul(win, r):
             k_win = window_of(k_bands[win // SPLIT][:], win % SPLIT)
-            sim = sim_banks.tile([P, TOKENS], F32, tag="sim")
+            early = win == 0 and r == ROW_TILES - 1
+            sim = (mx_banks if early else sim_banks).tile([P, TOKENS], F32, tag="mx" if early else "sim")
             for c in range(CK_TILES):
                 nc.tensor.matmul(
                     out=sim[:].rearrange("p (i j) -> p i j", j=WIN_COLS),
@@ -279,7 +284,7 @@ def tile_pyramidselfattentionblock_pa_kernel(tc, x, q, k, v_w, v_b, out):
             tiles[("e", win, r)] = e_rows
 
         def e_turn(win, half):
-            e_turned = turn_banks.tile([P, 2, HALF], F32, tag="turn")
+            e_turned = turn_bank(win if half else 0, [P, 2, HALF])
             for r in range(HALF // P):
                 e_words = tiles[("e", win, half * (HALF // P) + r)][:].bitcast(F32)
                 for u in range(2):
@@ -318,7 +323,7 @@ def tile_pyramidselfattentionblock_pa_kernel(tc, x, q, k, v_w, v_b, out):
             tiles[("inv", win)] = inv_sum
 
         def inv_turn(win):
-            inv_turned = turn_banks.tile([P, TOKENS], F32, tag="turn")
+            inv_turned = turn_bank(win, [P, TOKENS])
             for r in range(ROW_TILES):
                 nc.tensor.transpose(
                     out=inv_turned[:, r * P : (r + 1) * P],
@@ -372,8 +377,8 @@ def tile_pyramidselfattentionblock_pa_kernel(tc, x, q, k, v_w, v_b, out):
             if 0 <= win < N_WINDOWS:
                 stage(win, *args)
 
-        q_rows(0, 0, WIN_ROWS // ROW_TILES)
-        q_rows(0, WIN_ROWS // ROW_TILES, WIN_ROWS)
+        q_window(0)
+        q_window(1)
         last = N_WINDOWS - 1
         for c in range(-1, N_WINDOWS):
             run(sim_matmul, c, 1)
@@ -381,8 +386,6 @@ def tile_pyramidselfattentionblock_pa_kernel(tc, x, q, k, v_w, v_b, out):
             run(ctx_matmul, c - 2, 1)
             run(v_matmul_channels, c - 1)
             run(row_max, c, 0)
-            if c == 0:
-                q_window(1)
             run(exponent, c - 1, 3)
             run(e_copy, c - 1, 0)
             run(inv_copy, c - 2)
@@ -406,16 +409,17 @@ def tile_pyramidselfattentionblock_pa_kernel(tc, x, q, k, v_w, v_b, out):
             run(e_copy, c - 1, 1)
             if c == 0:
                 x_rows(nc.gpsimd, 0, 0, 8)
-                x_rows(nc.scalar, 0, 8, 16)
+                x_rows(nc.gpsimd, 0, 8, 12)
+                x_rows(nc.scalar, 0, 12, 16)
                 w_turn()
                 bias_spread()
+                w_copy()
 
             run(sim_matmul, c + 1, 0)
             run(e_turn, c, 0)
             run(inv_turn, c - 1)
             run(row_max, c, 3)
             if c == 0:
-                w_copy()
                 w_quantise()
             run(exponent, c, 2)
             run(v_copy, c - 1)
@@ -443,8 +447,8 @@ def tile_pyramidselfattentionblock_pa_kernel(tc, x, q, k, v_w, v_b, out):
         v_bias_channels(last)
         sum_invert(last)
         v_bias_keys(last)
-        v_turn(last)
         ctx_matmul(last - 1, 0)
+        v_turn(last)
         ctx_matmul(last - 1, 1)
         inv_copy(last - 1)
         v_copy(last)

from contextlib import ExitStack

import concourse.mybir as mybir
from concourse.masks import make_identity

F32 = mybir.dt.float32
BF16 = mybir.dt.bfloat16
U32 = mybir.dt.uint32
U8 = mybir.dt.uint8
FP8X4 = mybir.dt.float8_e4m3fn_x4
ADD = mybir.AluOpType.add
MULT = mybir.AluOpType.mult
MAX = mybir.AluOpType.max
IDENTITY = mybir.ActivationFunctionType.Identity
EXP = mybir.ActivationFunctionType.Exp
FREE_AXIS = mybir.AxisListType.X

P = 128
PACK = 4
IMAGES, CIN, CK, CV = 2, 512, 256, 256
SPLIT = 2
WIN_ROWS, WIN_COLS = 16, 32
TOKENS = WIN_ROWS * WIN_COLS
BAND = SPLIT * TOKENS
N_BANDS = IMAGES * SPLIT
N_WINDOWS = N_BANDS * SPLIT
CK_TILES = CK // P
CV_TILES = CV // P
ROW_TILES = TOKENS // P
BIAS_COLS = 4
GPSIMD_ROWS = 14
WARM_UPS = 6
ALL = slice(0, TOKENS)
HALF = TOKENS // 2

FLOPS = 2 * IMAGES * CV * CIN * SPLIT * BAND + 2 * 2 * N_WINDOWS * TOKENS * TOKENS * CK


def window_of(band_view, side):
    if band_view.ndim == 2:
        return band_view.rearrange("p (i d j) -> p d i j", d=SPLIT, j=WIN_COLS)[:, side]
    return band_view.rearrange("p c (i d j) -> p d c i j", d=SPLIT, j=WIN_COLS)[:, side]


def tile_pyramidselfattentionblock_pa_kernel(tc, x, q, k, v_w, v_b, out):
    nc = tc.nc
    with ExitStack() as ctx:
        ctx.enter_context(tc.manual_schedule())
        const = ctx.enter_context(tc.tile_pool(name="const", bufs=1))
        maps = ctx.enter_context(tc.tile_pool(name="maps", bufs=N_BANDS))
        work = ctx.enter_context(tc.tile_pool(name="work", bufs=3))
        q_pool = ctx.enter_context(tc.tile_pool(name="q_pool", bufs=4))
        x_pool = ctx.enter_context(tc.tile_pool(name="x_pool", bufs=1))
        rows = ctx.enter_context(tc.tile_pool(name="rows", bufs=2 * ROW_TILES))
        sim_banks = ctx.enter_context(tc.psum_pool(name="sim_banks", bufs=3))
        turn_banks = ctx.enter_context(tc.psum_pool(name="turn_banks", bufs=2))
        mx_banks = ctx.enter_context(tc.psum_pool(name="mx_banks", bufs=3))

        w_raw = const.tile([P, CV_TILES, CIN], BF16)
        bias_row = const.tile([P, CV], BF16)
        nc.gpsimd.memset(bias_row[:], 0.0)
        zeros = const.tile([P, TOKENS], BF16)
        nc.vector.memset(zeros[:], 0.0)
        ones = const.tile([P, P], BF16)
        nc.gpsimd.memset(ones[:], 1.0)
        q_bands, k_bands, x_bands = [], [], []
        for band in range(N_BANDS):
            image, pixels = band // SPLIT, slice((band % SPLIT) * BAND, (band % SPLIT + 1) * BAND)
            q_map = q[image].rearrange("(c p) h w -> p c (h w)", p=P)[:, :, pixels]
            k_map = k[image].rearrange("(c p) h w -> p c (h w)", p=P)[:, :, pixels]
            x_map = x[image].rearrange("(p j) h w -> p j (h w)", j=PACK)[:, :, pixels]
            q_raw = maps.tile([P, CK_TILES, BAND], BF16)
            k_raw = maps.tile([P, CK_TILES, BAND], BF16)
            x_raw = maps.tile([P, PACK, BAND], BF16)
            if band == 0:
                nc.sync.dma_start(out=q_raw[:], in_=q_map)
                nc.sync.dma_start(out=k_raw[:], in_=k_map)
                upper, lower = slice(0, BAND // 2), slice(BAND // 2, BAND)
                nc.sync.dma_start(out=x_raw[:, :, upper], in_=x_map[:, :, upper])
                nc.sync.dma_start(out=w_raw[:], in_=v_w.rearrange("(h p) c -> p h c", p=P))
                nc.sync.dma_start(out=x_raw[:, :, lower], in_=x_map[:, :, lower])
                nc.sync.dma_start(out=bias_row[0:1, :], in_=v_b.rearrange("(u o) -> u o", u=1))
            else:
                nc.sync.dma_start(out=q_raw[:], in_=q_map)
                nc.sync.dma_start(out=k_raw[:], in_=k_map)
                nc.sync.dma_start(out=x_raw[:], in_=x_map)
            q_bands.append(q_raw)
            k_bands.append(k_raw)
            x_bands.append(x_raw)

        for w in range(WARM_UPS):
            warm = turn_banks.tile([P, TOKENS], F32, tag="turn")
            nc.tensor.matmul(out=warm[:], lhsT=zeros[:, :P], rhs=zeros[:], start=True, stop=True)

        ident_f32 = const.tile([P, P], F32)
        make_identity(nc, ident_f32[:])

        tiles = {}

        def w_turn():
            w_words = w_raw[:].bitcast(F32).rearrange("p h (w u) -> p h u w", u=2)
            w_turned = turn_banks.tile([P, 2, CV], F32, tag="turn")
            for h in range(CV_TILES):
                for u in range(2):
                    nc.tensor.transpose(out=w_turned[:, u, h * P : (h + 1) * P], in_=w_words[:, h, u, :], identity=ident_f32[:])
            tiles["wt"] = w_turned

        def w_copy():
            w_grouped = const.tile([P, CV * PACK], BF16, align_bytes=64)
            nc.vector.tensor_copy(
                out=w_grouped[:].bitcast(F32).rearrange("p (o u) -> p o u", u=2),
                in_=tiles["wt"][:].rearrange("p u o -> p o u"),
            )
            tiles["wg"] = w_grouped

        def w_quantise():
            w_codes = const.tile([P, CV], U32, align_bytes=64)
            w_scales = const.tile([P, CV], U8, align_bytes=64)
            nc.vector.quantize_mx(out=w_codes[:].bitcast(FP8X4), scales=w_scales[:], in_=tiles["wg"][:])
            tiles["wq"] = (w_codes, w_scales)

        def bias_spread():
            bias_acc = turn_banks.tile([P, P + BIAS_COLS], F32, tag="turn")
            nc.tensor.matmul(out=bias_acc[:, :P], lhsT=ones[:], rhs=bias_row[:, :P], start=True, stop=True)
            nc.tensor.matmul(out=bias_acc[:, P:], lhsT=bias_row[:, P:], rhs=ones[:, :BIAS_COLS], start=True, stop=True)
            tiles["bacc"] = bias_acc

        def bias_copy():
            bias = const.tile([P, P + BIAS_COLS], F32)
            nc.scalar.copy(out=bias[:], in_=tiles["bacc"][:])
            tiles["bias"] = bias

        def q_rows(win, top, bottom):
            if top == 0:
                tiles[("q", win)] = q_pool.tile([P, CK_TILES, TOKENS], BF16, name="q_win")
            engine = nc.vector if win < 2 else nc.gpsimd
            engine.tensor_scalar(
                out=tiles[("q", win)][:].rearrange("p c (i j) -> p c i j", j=WIN_COLS)[:, :, top:bottom],
                in0=window_of(q_bands[win // SPLIT][:], win % SPLIT)[:, :, top:bottom],
                scalar1=CK**-0.5,
                scalar2=0.0,
                op0=MULT,
                op1=ADD,
            )

        def q_window(win):
            q_rows(win, 0, WIN_ROWS)

        def x_rows(engine, win, top, bottom):
            if top == 0:
                tiles[("x", win)] = x_pool.tile([P, TOKENS, PACK], BF16, name="x_grouped", align_bytes=64)
            grouped = tiles[("x", win)][:].rearrange("p (i j) c -> p i j c", j=WIN_COLS)[:, top:bottom]
            raw = window_of(x_bands[win // SPLIT][:], win % SPLIT).rearrange("p c i j -> p i j c")[:, top:bottom]
            if engine == nc.scalar:
                nc.scalar.copy(out=grouped, in_=raw)
            elif engine == nc.vector:
                nc.vector.tensor_copy(out=grouped, in_=raw)
            else:
                nc.gpsimd.tensor_scalar(out=grouped, in0=raw, scalar1=1.0, scalar2=0.0, op0=MULT, op1=ADD)

        def x_gpsimd(win):
            x_rows(nc.gpsimd, win, 0, GPSIMD_ROWS)

        def x_scalar(win):
            x_rows(nc.scalar, win, GPSIMD_ROWS, WIN_ROWS)

        def x_quantise(win):
            x_codes = work.tile([P, TOKENS], U32, align_bytes=64)
            x_scales = work.tile([P, TOKENS], U8, align_bytes=64)
            nc.vector.quantize_mx(
                out=x_codes[:].bitcast(FP8X4), scales=x_scales[:], in_=tiles[("x", win)][:].rearrange("p l c -> p (l c)")
            )
            tiles[("xq", win)] = (x_codes, x_scales)

        def v_matmul_keys(win):
            x_codes, x_scales = tiles[("xq", win)]
            w_codes, w_scales = tiles["wq"]
            v_acc = mx_banks.tile([P, PACK, P], F32, tag="mx")
            for t in range(PACK):
                keys = slice(t * P, (t + 1) * P)
                nc.tensor.matmul_mx(
                    out=v_acc[:, t, :],
                    lhsT=x_codes[:, keys].bitcast(FP8X4),
                    lhsT_scale=x_scales[:, keys],
                    rhs=w_codes[:, :P].bitcast(FP8X4),
                    rhs_scale=w_scales[:, :P],
                    start=True,
                    stop=True,
                )
            tiles[("vacc", win, 0)] = v_acc
            tiles[("vg", win)] = work.tile([P, CV, PACK], BF16, name="v_grouped", align_bytes=64)

        def v_bias_keys(win):
            nc.vector.tensor_tensor(
                out=tiles[("vg", win)][:, :P],
                in0=tiles[("vacc", win, 0)][:].rearrange("p t o -> p o t"),
                in1=tiles["bias"][:, :P].unsqueeze(2).to_broadcast([P, P, PACK]),
                op=ADD,
            )

        def v_matmul_channels(win):
            x_codes, x_scales = tiles[("xq", win)]
            w_codes, w_scales = tiles["wq"]
            v_acc = mx_banks.tile([P, TOKENS], F32, tag="mx")
            nc.tensor.matmul_mx(
                out=v_acc[:],
                lhsT=w_codes[:, P:].bitcast(FP8X4),
                lhsT_scale=w_scales[:, P:],
                rhs=x_codes[:].bitcast(FP8X4),
                rhs_scale=x_scales[:],
                start=True,
                stop=True,
            )
            tiles[("vacc", win, 1)] = v_acc

        def v_bias_channels(win):
            v_rows = rows.tile([P, TOKENS], BF16)
            nc.scalar.activation(
                out=v_rows[:].rearrange("p (u k e) -> p u k e", u=2, e=2),
                in_=tiles[("vacc", win, 1)][:].rearrange("p (u e k) -> p u k e", u=2, e=2),
                func=IDENTITY,
                bias=tiles["bias"][:, P : P + 1],
                scale=1.0,
            )
            tiles[("v", win)] = v_rows

        def turn_bank(win, shape):
            if win == N_WINDOWS - 1:
                return sim_banks.tile(shape, F32, name="turned", tag="sim")
            return turn_banks.tile(shape, F32, name="turned", tag="turn")

        def v_turn(win):
            v_turned = turn_bank(win, [P, 2, P])
            v_words = tiles[("v", win)][:].bitcast(F32)
            for u in range(2):
                nc.tensor.transpose(out=v_turned[:, u, :], in_=v_words[:, u * P : (u + 1) * P], identity=ident_f32[:])
            tiles[("vt", win)] = v_turned

        def v_copy(win):
            words = tiles[("vg", win)][:].rearrange("p o t -> p (o t)").bitcast(F32).rearrange("p (o u) -> p o u", u=2)
            nc.scalar.copy(out=words[:, P:], in_=tiles[("vt", win)][:].rearrange("p u o -> p o u"))

        def v_quantise(win):
            v_codes = work.tile([P, CV], U32, align_bytes=64)
            v_scales = work.tile([P, CV], U8, align_bytes=64)
            nc.vector.quantize_mx(
                out=v_codes[:].bitcast(FP8X4), scales=v_scales[:], in_=tiles[("vg", win)][:].rearrange("p o t -> p (o t)")
            )
            tiles[("vq", win)] = (v_codes, v_scales)

        def sim_matmul(win, r):
            k_win = window_of(k_bands[win // SPLIT][:], win % SPLIT)
            early = win == 0 and r == ROW_TILES - 1
            sim = (mx_banks if early else sim_banks).tile([P, TOKENS], F32, tag="mx" if early else "sim")
            for c in range(CK_TILES):
                nc.tensor.matmul(
                    out=sim[:].rearrange("p (i j) -> p i j", j=WIN_COLS),
                    lhsT=tiles[("q", win)][:, c, r * P : (r + 1) * P],
                    rhs=k_win[:, c],
                    start=(c == 0),
                    stop=(c == CK_TILES - 1),
                )
            tiles[("sim", win, r)] = sim

        def row_max(win, r):
            if r == 0:
                tiles[("max", win)] = work.tile([P, ROW_TILES], F32, name="neg_max")
            nc.vector.tensor_reduce(
                out=tiles[("max", win)][:, r : r + 1], in_=tiles[("sim", win, r)][:], axis=FREE_AXIS, op=MAX, negate=True
            )

        def exponent(win, r):
            if r == 0:
                tiles[("sum", win)] = work.tile([P, ROW_TILES], F32, name="row_sum")
            e_rows = rows.tile([P, TOKENS], BF16)
            nc.scalar.activation(
                out=e_rows[:].rearrange("p (u k e) -> p u k e", u=2, e=2),
                in_=tiles[("sim", win, r)][:].rearrange("p (u e k) -> p u k e", u=2, e=2),
                func=EXP,
                bias=tiles[("max", win)][:, r : r + 1],
                scale=1.0,
                accum_out=tiles[("sum", win)][:, r : r + 1],
            )
            tiles[("e", win, r)] = e_rows

        def e_turn(win, half):
            e_turned = turn_bank(win if half else 0, [P, 2, HALF])
            for r in range(HALF // P):
                e_words = tiles[("e", win, half * (HALF // P) + r)][:].bitcast(F32)
                for u in range(2):
                    nc.tensor.transpose(
                        out=e_turned[:, u, r * P : (r + 1) * P],
                        in_=e_words[:, u * P : (u + 1) * P],
                        identity=ident_f32[:],
                    )
            tiles[("et", win, half)] = e_turned

        def e_copy(win, half):
            if half == 0:
                tiles[("eg", win)] = work.tile([P, TOKENS, PACK], BF16, name="e_grouped", align_bytes=64)
            e_grouped = tiles[("eg", win)][:].rearrange("p l t -> p (l t)").bitcast(F32).rearrange("p (l u) -> p l u", u=2)
            nc.scalar.copy(
                out=e_grouped[:, half * HALF : (half + 1) * HALF, :],
                in_=tiles[("et", win, half)][:].rearrange("p u l -> p l u"),
            )

        def e_quantise(win, part=ALL):
            if part.start == 0:
                tiles[("eq", win)] = (
                    work.tile([P, TOKENS], U32, name="e_codes", align_bytes=64),
                    work.tile([P, TOKENS], U8, name="e_scales", align_bytes=64),
                )
            e_codes, e_scales = tiles[("eq", win)]
            nc.vector.quantize_mx(
                out=e_codes[:, part].bitcast(FP8X4),
                scales=e_scales[:, part],
                in_=tiles[("eg", win)][:, part].rearrange("p l t -> p (l t)"),
            )

        def sum_invert(win):
            inv_sum = work.tile([P, ROW_TILES], F32)
            nc.vector.reciprocal(out=inv_sum[:], in_=tiles[("sum", win)][:])
            tiles[("inv", win)] = inv_sum

        def inv_turn(win):
            inv_turned = turn_bank(win, [P, TOKENS])
            for r in range(ROW_TILES):
                nc.tensor.transpose(
                    out=inv_turned[:, r * P : (r + 1) * P],
                    in_=tiles[("inv", win)][:, r : r + 1].to_broadcast([P, P]),
                    identity=ident_f32[:],
                )
            tiles[("invt", win)] = inv_turned

        def inv_copy(win):
            inv_all = work.tile([P, TOKENS], F32)
            nc.scalar.copy(out=inv_all[:], in_=tiles[("invt", win)][:])
            tiles[("inva", win)] = inv_all

        def ctx_matmul(win, h, part=ALL):
            v_codes, v_scales = tiles[("vq", win)]
            e_codes, e_scales = tiles[("eq", win)]
            if part.start == 0:
                ctx_acc = mx_banks.tile([P, TOKENS], F32, tag="mx")
            else:
                ctx_acc = sim_banks.tile([P, TOKENS], F32, tag="sim")
            tiles[("ctx", win, h, part.start)] = ctx_acc
            nc.tensor.matmul_mx(
                out=ctx_acc[:, part],
                lhsT=v_codes[:, h * P : (h + 1) * P].bitcast(FP8X4),
                lhsT_scale=v_scales[:, h * P : (h + 1) * P],
                rhs=e_codes[:, part].bitcast(FP8X4),
                rhs_scale=e_scales[:, part],
                start=True,
                stop=True,
            )

        def ctx_scale(win, h, part=ALL):
            band, side = win // SPLIT, win % SPLIT
            if side == 0:
                tiles[("out", band, h)] = work.tile([P, BAND], F32, name="out_band%d" % h)
            top, bottom = part.start // WIN_COLS, part.stop // WIN_COLS
            nc.vector.tensor_tensor(
                out=window_of(tiles[("out", band, h)][:], side)[:, top:bottom],
                in0=tiles[("ctx", win, h, part.start)][:, part].rearrange("p (i j) -> p i j", j=WIN_COLS),
                in1=tiles[("inva", win)][:, part].rearrange("p (i j) -> p i j", j=WIN_COLS),
                op=MULT,
            )
            if side == SPLIT - 1:
                image, first_row = band // SPLIT, (band % SPLIT) * WIN_ROWS
                nc.sync.dma_start(
                    out=out[image, h * P : (h + 1) * P, first_row + top : first_row + bottom, :].rearrange("o h w -> o (h w)"),
                    in_=tiles[("out", band, h)][:, SPLIT * part.start : SPLIT * part.stop],
                )

        def run(stage, win, *args):
            if 0 <= win < N_WINDOWS:
                stage(win, *args)

        q_window(0)
        q_window(1)
        last = N_WINDOWS - 1
        for c in range(-1, N_WINDOWS):
            run(sim_matmul, c, 1)
            run(ctx_matmul, c - 2, 0)
            run(ctx_matmul, c - 2, 1)
            run(v_matmul_channels, c - 1)
            run(row_max, c, 0)
            run(exponent, c - 1, 3)
            run(e_copy, c - 1, 0)
            run(inv_copy, c - 2)

            run(sim_matmul, c, 2)
            run(e_turn, c - 1, 1)
            run(row_max, c, 1)
            run(ctx_scale, c - 2, 0)
            if c > 1:
                run(x_scalar, c)
            run(exponent, c, 0)
            run(v_bias_channels, c - 1)

            run(sim_matmul, c, 3)
            run(v_matmul_keys, c - 1)
            run(v_turn, c - 1)
            run(row_max, c, 2)
            run(ctx_scale, c - 2, 1)
            run(sum_invert, c - 1)
            run(exponent, c, 1)
            run(e_copy, c - 1, 1)
            if c == 0:
                x_rows(nc.gpsimd, 0, 0, 8)
                x_rows(nc.gpsimd, 0, 8, 12)
                x_rows(nc.scalar, 0, 12, 16)
                w_turn()
                bias_spread()
                w_copy()

            run(sim_matmul, c + 1, 0)
            run(e_turn, c, 0)
            run(inv_turn, c - 1)
            run(row_max, c, 3)
            if c == 0:
                w_quantise()
            run(exponent, c, 2)
            run(v_copy, c - 1)
            if c == last:
                x_quantise(last)
            run(v_bias_keys, c - 1)
            run(e_quantise, c - 1)
            run(v_quantise, c - 1)
            if c < last:
                run(x_quantise, c)
            if c == 0:
                bias_copy()
                q_window(2)
            if c >= 0:
                if c == 0:
                    x_rows(nc.gpsimd, 1, 0, 16)
                else:
                    run(x_gpsimd, c + 1)
                run(q_window, c + 3)

        halves = (slice(0, HALF), slice(HALF, TOKENS))
        v_matmul_channels(last)
        v_matmul_keys(last)
        exponent(last, 3)
        v_bias_channels(last)
        sum_invert(last)
        v_bias_keys(last)
        ctx_matmul(last - 1, 0)
        v_turn(last)
        ctx_matmul(last - 1, 1)
        inv_copy(last - 1)
        v_copy(last)
        ctx_scale(last - 1, 0)
        e_turn(last, 1)
        inv_turn(last)
        e_copy(last, 0)
        e_copy(last, 1)
        inv_copy(last)
        v_quantise(last)
        e_quantise(last, halves[0])
        ctx_scale(last - 1, 1)
        for h in range(CV_TILES):
            ctx_matmul(last, h, halves[0])
        e_quantise(last, halves[1])
        for h in range(CV_TILES):
            ctx_scale(last, h, halves[0])
            ctx_matmul(last, h, halves[1])
        for h in range(CV_TILES):
            ctx_scale(last, h, halves[1])
